import numpy as np
import ml_dtypes


def mxq(x, axis, fmt="e4m3"):
    dtype, down = {"e4m3": (ml_dtypes.float8_e4m3fn, 7), "e5m2": (ml_dtypes.float8_e5m2, 14)}[fmt]
    v = np.moveaxis(np.asarray(x, np.float32).astype(ml_dtypes.bfloat16).astype(np.float64), axis, -1)
    blocks = v.reshape(v.shape[:-1] + (-1, 32))
    amax = np.abs(blocks).max(-1, keepdims=True)
    byte = np.maximum(np.where(amax > 0, np.frexp(amax)[1] - 1 + 127, 0) - down, 1)
    scale = np.exp2(byte - 127.0)
    codes = (blocks / scale).astype(np.float32).astype(dtype).astype(np.float64)
    return np.moveaxis((codes * scale).reshape(v.shape), -1, axis)


WIDE = False


def mx_kscale(k):
    if not WIDE:
        return np.ones(k)
    levels = np.array([18, -18])
    if k % 512:
        return np.exp2(np.random.permutation(np.resize(levels, k // 32))).repeat(32)
    a = np.empty((k // 512, 16))
    for p in range(k // 512):
        a[p, :8] = np.random.permutation(np.resize(levels, 8))
        for g in range(8):
            far = levels[np.abs(levels - a[p, g]) >= 10]
            a[p, g + 8] = far[np.random.randint(len(far))]
    return np.exp2(a.ravel()).repeat(32)


BF16 = ml_dtypes.bfloat16


def bf(x):
    return np.asarray(x, np.float32).astype(BF16)


def f64(x):
    return np.asarray(x).astype(np.float64)


B, S, D, F = 2, 512, 1024, 2048
EPS = 1e-6


def yat_scale(alpha, nf):
    return (np.sqrt(nf) / np.log(1.0 + nf)) ** f64(alpha)


def setup_inputs():
    s = mx_kscale(B * S).reshape(B, S, 1)
    u = mx_kscale(F)
    x0 = bf(0.25 + 0.5 * np.random.standard_normal((B, S, D)))
    w0 = bf(0.25 + 0.5 * np.random.standard_normal((F, D)))
    alpha = bf(1.0 + 0.1 * np.random.standard_normal(1))
    bias = bf(0.1 * np.random.standard_normal(F))
    g = bf(np.random.standard_normal((B, S, F)) * np.exp2(np.random.randint(-6, 1, (B, S, 1))) / s * u)
    y = f64(x0) @ f64(w0).T
    x_sq = np.sum(f64(x0) ** 2, axis=-1, keepdims=True)
    w_sq = np.sum(f64(w0) ** 2, axis=-1)
    return {"x": bf(f64(x0) * s),
            "weight": bf(f64(w0) / u[:, None]),
            "alpha": alpha,
            "bias": bias,
            "y": np.asarray(y, np.float32),
            "x_sq": np.asarray(x_sq, np.float32),
            "w_sq": np.asarray(w_sq, np.float32),
            "grad_out": g}


def reference(x, weight, alpha, bias, y, x_sq, w_sq, grad_out):
    nb, ns, nd = x.shape
    nf = weight.shape[0]
    xf = f64(x).reshape(nb * ns, nd)
    wf = f64(weight)
    yf = f64(y).reshape(nb * ns, nf)
    dist = f64(x_sq).reshape(nb * ns, 1) + f64(w_sq) - 2.0 * yf
    r = yf / (dist + EPS)
    gs = f64(grad_out).reshape(nb * ns, nf) * yat_scale(alpha, nf)
    dy = 2.0 * gs * r * (1.0 + r)
    ddist = -gs * r * r
    dx = mxq(dy, 1, "e5m2") @ mxq(wf, 0, "e4m3")
    dx = dx + 2.0 * xf * np.sum(ddist, axis=1, keepdims=True)
    dw = mxq(dy, 0, "e5m2").T @ mxq(xf, 0, "e4m3")
    dw = dw + 2.0 * wf * np.sum(ddist, axis=0)[:, None]
    return dx.reshape(nb, ns, nd), dw

@@ -1,0 +1,324 @@
+import math
+from contextlib import ExitStack
+
+import concourse.mybir as mybir
+from concourse.masks import make_identity
+
+B, S, D, F = 2, 512, 1024, 2048
+FLOPS = 2 * 2 * B * S * D * F
+BYTES = 2 * B * S * D + 2 * F * D + 2 * B * S * F + 4 * B * S * F + 4 * (B * S + F) + 2 + 4 * B * S * D + 4 * F * D
+
+P = 128
+J = 4
+H = 4
+FB = 512
+NT = 512
+EPS = 1e-6
+LOG_BASE = math.log(math.sqrt(F) / math.log(1.0 + F))
+
+F32 = mybir.dt.float32
+BF16 = mybir.dt.bfloat16
+U32 = mybir.dt.uint32
+U8 = mybir.dt.uint8
+E4M3 = mybir.dt.float8_e4m3fn_x4
+E5M2 = mybir.dt.float8_e5m2_x4
+ACT = mybir.ActivationFunctionType
+ALU = mybir.AluOpType
+AX = mybir.AxisListType
+
+PAIRS = H * B * 2
+Z_ON_GPSIMD = tuple(range(2, 16))
+MX_BANKS = 3
+
+
+def tile_yatdense_v_kernel(tc, x, weight, alpha, bias, y, x_sq, w_sq, grad_out, out_0, out_1):
+    nc = tc.nc
+    x_v = x.rearrange("g (p j) d -> p g j d", j=J)
+    w_v = weight.rearrange("(h p j) d -> p h j d", h=H, j=J)
+    y_v = y.rearrange("g (p j) f -> p g j f", j=J)
+    g_v = grad_out.rearrange("g (p j) f -> p g j f", j=J)
+    o0_v = out_0.rearrange("g (p j) d -> p g j d", j=J)
+    o1_v = out_1.rearrange("(h p j) d -> p h j d", h=H, j=J)
+
+    with ExitStack() as ctx:
+        keep = ctx.enter_context(tc.tile_pool(name="keep", bufs=1))
+        io = ctx.enter_context(tc.tile_pool(name="io", bufs=4))
+        work = ctx.enter_context(tc.tile_pool(name="work", bufs=2))
+        psum = ctx.enter_context(tc.psum_pool(name="psum", bufs=1))
+
+        ident = keep.tile([P, P], F32, name="ident")
+        wcol = keep.tile([P, H, J], F32, name="wcol")
+        xsq = keep.tile([P, B, J], F32, name="xsq")
+        xse = keep.tile([P, B, J], F32, name="xse")
+        al = keep.tile([P, 1], BF16, name="al")
+        sc = keep.tile([P, 1], F32, name="sc")
+        s2 = keep.tile([P, 1], F32, name="s2")
+        ns2 = keep.tile([P, 1], F32, name="ns2")
+        w2b = keep.tile([P, H, FB], F32, name="w2b")
+        acc_f = keep.tile([P, B, J, H], F32, name="acc_f")
+        tau = keep.tile([P, B, J], F32, name="tau")
+        taus = keep.tile([P, B, J], F32, name="taus")
+        sig = keep.tile([P, H, J], F32, name="sig")
+        sigs = keep.tile([P, H, J], F32, name="sigs")
+        x_raw = keep.tile([P, B, J, D], BF16, name="x_raw")
+        w_codes = keep.tile([P, H, D], U32, name="w_codes", align_bytes=64)
+        w_scales = keep.tile([P, H, D], U8, name="w_scales", align_bytes=64)
+        x_codes = keep.tile([P, B, D], U32, name="x_codes", align_bytes=64)
+        x_scales = keep.tile([P, B, D], U8, name="x_scales", align_bytes=64)
+        f_codes = keep.tile([P, H, B * J * P], U32, name="f_codes", align_bytes=64)
+        f_scales = keep.tile([P, H, B * J * P], U8, name="f_scales", align_bytes=64)
+
+        def where(i):
+            h, rest = divmod(i, 4)
+            g, jp = divmod(rest, 2)
+            return h, g, jp
+
+        yt, gt, zt, qt, rt, mt, nt, dyf, dyt, bk, tcod, wraw, stg = {}, {}, {}, {}, {}, {}, {}, {}, {}, {}, {}, {}, {}
+        sums = {}
+
+        def load_pair(i):
+            h, g, jp = where(i)
+            y_tile = io.tile([P, 2, FB], F32, name="y_tile", bufs=4)
+            g_tile = io.tile([P, 2, FB], BF16, name="g_tile", bufs=5)
+            yt[i], gt[i] = y_tile, g_tile
+            nc.sync.dma_start(out=y_tile[:], in_=y_v[:, g, 2 * jp:2 * jp + 2, h * FB:(h + 1) * FB])
+            nc.sync.dma_start(out=g_tile[:], in_=g_v[:, g, 2 * jp:2 * jp + 2, h * FB:(h + 1) * FB])
+
+        def load_w(h):
+            w_tile = io.tile([P, J, D], BF16, name="w_tile", bufs=4)
+            wraw[h] = w_tile
+            nc.sync.dma_start(out=w_tile[:], in_=w_v[:, h])
+
+        def op_z(i):
+            h, g, jp = where(i)
+            z_tile = work.tile([P, 2, FB], F32, name="z_tile", bufs=3)
+            zt[i] = z_tile
+            eng = nc.gpsimd if i in Z_ON_GPSIMD else nc.vector
+            eng.tensor_tensor(out=z_tile[:], in0=yt[i][:], in1=w2b[:, h:h + 1, :].to_broadcast([P, 2, FB]), op=ALU.subtract)
+
+        def op_q(i):
+            h, g, jp = where(i)
+            q_tile = work.tile([P, 2, FB], F32, name="q_tile", bufs=2)
+            qt[i] = q_tile
+            for s in range(2):
+                nc.scalar.activation(
+                    out=q_tile[:, s, :].rearrange("p (t m) -> p t m", t=J),
+                    in_=zt[i][:, s, :].rearrange("p (m t) -> p t m", t=J),
+                    func=ACT.Abs_reciprocal_sqrt, bias=xse[:, g, 2 * jp + s:2 * jp + s + 1], scale=-2.0)
+            nc.scalar.activation(out=q_tile[:], in_=q_tile[:], func=ACT.Square)
+
+        def op_r(i):
+            r_tile = work.tile([P, 2, FB], F32, name="r_tile", bufs=2)
+            rt[i] = r_tile
+            nc.vector.tensor_tensor(
+                out=r_tile[:].rearrange("p s (t m) -> p s t m", t=J),
+                in0=yt[i][:].rearrange("p s (m t) -> p s t m", t=J),
+                in1=qt[i][:].rearrange("p s (t m) -> p s t m", t=J), op=ALU.mult)
+
+        def op_m(i):
+            m_tile = work.tile([P, 2, FB], F32, name="m_tile", bufs=2)
+            mt[i] = m_tile
+            nc.vector.tensor_tensor(
+                out=m_tile[:].rearrange("p s (t m) -> p s t m", t=J),
+                in0=rt[i][:].rearrange("p s (t m) -> p s t m", t=J),
+                in1=gt[i][:].rearrange("p s (m t) -> p s t m", t=J), op=ALU.mult)
+
+        def op_n(i, s):
+            h, g, jp = where(i)
+            if s == 0:
+                n_tile = work.tile([P, 2, FB], F32, name="n_tile", bufs=5)
+                nt[i] = n_tile
+            nc.vector.scalar_tensor_tensor(
+                out=nt[i][:, s, :], in0=mt[i][:, s, :], scalar=1.0, in1=rt[i][:, s, :],
+                op0=ALU.mult, op1=ALU.mult, accum_out=acc_f[:, g, 2 * jp + s, h:h + 1])
+
+        def op_fwd(i):
+            f_tile = work.tile([P, 2, P, J], BF16, name="f_tile", bufs=3, align_bytes=64)
+            dyf[i] = f_tile
+            for s in range(2):
+                pf = psum.tile([P, J, P], F32, name="pf", bufs=2)
+                for t in range(J):
+                    cols = slice(t * P, (t + 1) * P)
+                    nc.tensor.matmul(out=pf[:, t, :], lhsT=mt[i][:, s, cols], rhs=ident[:], is_transpose=True, start=True, stop=False)
+                    nc.tensor.matmul(out=pf[:, t, :], lhsT=nt[i][:, s, cols], rhs=ident[:], is_transpose=True, start=False, stop=True)
+                nc.scalar.activation(out=f_tile[:, s], in_=pf[:].rearrange("p t k -> p k t"), func=ACT.Copy, scale=s2[:, 0:1])
+
+        def op_qf(i):
+            h, g, jp = where(i)
+            c0 = (g * J + 2 * jp) * P
+            nc.vector.quantize_mx(
+                out=f_codes[:, h, c0:c0 + 2 * P].bitcast(E5M2), scales=f_scales[:, h, c0:c0 + 2 * P],
+                in_=dyf[i][:].rearrange("p s k t -> p (s k t)"))
+
+        def op_back(i):
+            h, g, jp = where(i)
+            if jp == 0:
+                b0 = psum.tile([P, J * P], F32, name="b0", bufs=1)
+                b1 = psum.tile([P, J * P], F32, name="b1", bufs=1)
+                bk[i // 2] = (b0, b1)
+            for s in range(2):
+                words = dyf[i][:, s].rearrange("p k t -> p (k t)").bitcast(F32)
+                for e in range(2):
+                    j = 2 * jp + s
+                    nc.tensor.transpose(bk[i // 2][e][:, j * P:(j + 1) * P], words[:, e:2 * P:2], ident[:])
+
+        def op_back_copy(u):
+            t_tile = work.tile([P, J, P, J], BF16, name="t_tile", bufs=2, align_bytes=64)
+            dyt[u] = t_tile
+            for e in range(2):
+                nc.scalar.copy(out=t_tile[:, 2 * e:2 * e + 2],
+                               in_=bk[u][e][:].bitcast(BF16).rearrange("p (j m i) -> p i m j", j=J, i=2))
+
+        def op_qt(u):
+            t_codes = work.tile([P, FB], U32, name="t_codes", bufs=4, align_bytes=64)
+            t_scales = work.tile([P, FB], U8, name="t_scales", bufs=4, align_bytes=64)
+            tcod[u] = (t_codes, t_scales)
+            nc.vector.quantize_mx(out=t_codes[:].bitcast(E5M2), scales=t_scales[:], in_=dyt[u][:].rearrange("p t m j -> p (t m j)"))
+
+        def op_sum(h):
+            ps = psum.tile([P, J, P], F32, name="ps", bufs=1)
+            sums[h] = ps
+            for t in range(J):
+                for k in range(8):
+                    i, s = 4 * h + k // 2, k % 2
+                    nc.tensor.matmul(out=ps[:, t, :], lhsT=nt[i][:, s, t * P:(t + 1) * P], rhs=ident[:], is_transpose=True, start=(k == 0), stop=(k == 7))
+
+        def op_sum_reduce(h):
+            nc.vector.tensor_reduce(out=sig[:, h, :], in_=sums[h][:], axis=AX.X, op=ALU.add)
+            nc.vector.tensor_scalar(out=sigs[:, h, :], in0=sig[:, h, :], scalar1=ns2[:, 0:1], scalar2=None, op0=ALU.mult)
+
+        def op_tau(i):
+            h, g, jp = where(i)
+            nc.vector.tensor_reduce(out=tau[:, g, 2 * jp:2 * jp + 2], in_=acc_f[:, g, 2 * jp:2 * jp + 2, :], axis=AX.X, op=ALU.add)
+            nc.vector.tensor_scalar(out=taus[:, g, 2 * jp:2 * jp + 2], in0=tau[:, g, 2 * jp:2 * jp + 2], scalar1=ns2[:, 0:1], scalar2=None, op0=ALU.mult)
+
+        pieces = [("x", g, n) for g in range(B) for n in range(2)] + [("w", h, n) for h in range(H) for n in range(2)]
+
+        def op_stage(k):
+            kind, a, n = pieces[k]
+            s_tile = work.tile([P, NT, J], BF16, name="s_tile", bufs=2, align_bytes=64)
+            stg[k] = s_tile
+            src = x_raw[:, a, :, n * NT:(n + 1) * NT] if kind == "x" else wraw[a][:, :, n * NT:(n + 1) * NT]
+            nc.scalar.copy(out=s_tile[:], in_=src.rearrange("p j d -> p d j"))
+
+        def op_stage_q(k):
+            kind, a, n = pieces[k]
+            codes, scales = (x_codes, x_scales) if kind == "x" else (w_codes, w_scales)
+            nc.vector.quantize_mx(out=codes[:, a, n * NT:(n + 1) * NT].bitcast(E4M3), scales=scales[:, a, n * NT:(n + 1) * NT],
+                                  in_=stg[k][:].rearrange("p d j -> p (d j)"))
+
+        ready = []
+        pending = []
+        outs = {}
+
+        def emit_mm():
+            kind, a, b, n = ready.pop(0)
+            acc = psum.tile([P, NT], F32, name="acc", bufs=MX_BANKS)
+            cols = slice(n * NT, (n + 1) * NT)
+            if kind == 1:
+                for g in range(B):
+                    codes, scales = tcod[2 * a + g]
+                    nc.tensor.matmul_mx(out=acc[:], lhsT=codes[:, b * P:(b + 1) * P].bitcast(E5M2), lhsT_scale=scales[:, b * P:(b + 1) * P],
+                                        rhs=x_codes[:, g, cols].bitcast(E4M3), rhs_scale=x_scales[:, g, cols], start=(g == 0), stop=(g == B - 1))
+            else:
+                toks = slice((a * J + b) * P, (a * J + b + 1) * P)
+                for h in range(H):
+                    nc.tensor.matmul_mx(out=acc[:], lhsT=f_codes[:, h, toks].bitcast(E5M2), lhsT_scale=f_scales[:, h, toks],
+                                        rhs=w_codes[:, h, cols].bitcast(E4M3), rhs_scale=w_scales[:, h, cols], start=(h == 0), stop=(h == H - 1))
+            pending.append((kind, a, b, n, acc))
+
+        def emit_stt():
+            kind, a, b, n, acc = pending.pop(0)
+            cols = slice(n * NT, (n + 1) * NT)
+            if n == 0:
+                o_tile = io.tile([P, D], F32, name="o_tile", bufs=3)
+                outs[(kind, a, b)] = o_tile
+            o = outs[(kind, a, b)]
+            if kind == 1:
+                raw, fac, dst = wraw[a][:, b, cols], sigs[:, a, b:b + 1], o1_v[:, a, b]
+            else:
+                raw, fac, dst = x_raw[:, a, b, cols], taus[:, a, b:b + 1], o0_v[:, a, b]
+            nc.vector.scalar_tensor_tensor(out=o[:, cols], in0=raw, scalar=fac, in1=acc[:], op0=ALU.mult, op1=ALU.add)
+            if n == 1:
+                nc.sync.dma_start(out=dst, in_=o[:])
+
+        def some_stt():
+            if pending:
+                emit_stt()
+
+        with tc.manual_schedule():
+            nc.sync.dma_start(out=wcol[:], in_=w_sq.rearrange("(h m t) -> m h t", h=H, t=J))
+            nc.sync.dma_start(out=xsq[:], in_=x_sq.rearrange("g (p j) o -> p g (j o)", j=J))
+            nc.sync.dma_start(out=al[:], in_=alpha.partition_broadcast(P))
+            make_identity(nc, ident[:])
+            load_pair(0)
+            load_pair(1)
+            nc.scalar.activation(out=sc[:], in_=al[:], func=ACT.Exp, scale=LOG_BASE)
+            nc.vector.tensor_scalar(out=xse[:], in0=xsq[:], scalar1=EPS, scalar2=None, op0=ALU.add)
+            for h in range(H):
+                pw = psum.tile([P, J, P], F32, name="pf", bufs=2)
+                for t in range(J):
+                    nc.tensor.transpose(pw[:, t, :], wcol[:, h, t:t + 1].to_broadcast([P, P]), ident[:])
+                nc.scalar.activation(out=w2b[:, h, :].rearrange("p (m t) -> p m t", t=J), in_=pw[:].rearrange("p t m -> p m t"), func=ACT.Copy, scale=0.5)
+            nc.vector.tensor_scalar(out=s2[:], in0=sc[:], scalar1=2.0, scalar2=None, op0=ALU.mult)
+            nc.vector.tensor_scalar(out=ns2[:], in0=sc[:], scalar1=-2.0, scalar2=None, op0=ALU.mult)
+            nc.sync.dma_start(out=x_raw[:, 0], in_=x_v[:, 0])
+            load_pair(2)
+            nc.sync.dma_start(out=x_raw[:, 1], in_=x_v[:, 1])
+            load_pair(3)
+            op_z(0)
+            op_z(1)
+            op_q(0)
+            last = PAIRS + 3
+            for i in range(last):
+                live = i < PAIRS
+                if 1 <= i and i + 3 < PAIRS:
+                    load_pair(i + 3)
+                if 1 <= i <= 4:
+                    load_w(i - 1)
+                if i + 1 < PAIRS:
+                    op_q(i + 1)
+                if live:
+                    op_r(i)
+                if 2 <= i < PAIRS + 2:
+                    op_back(i - 2)
+                if 1 <= i < PAIRS + 1:
+                    op_fwd(i - 1)
+                if 2 <= i < PAIRS + 2:
+                    op_qf(i - 2)
+                    if i - 2 >= PAIRS - 4:
+                        op_tau(i - 2)
+                        h, g, jp = where(i - 2)
+                        ready.extend([(0, g, 2 * jp + s, n) for s in range(2) for n in range(2)])
+                if i + 2 < PAIRS:
+                    op_z(i + 2)
+                if live:
+                    op_m(i)
+                if 2 <= i < PAIRS + 2 and i % 2 == 1:
+                    op_back_copy((i - 2) // 2)
+                some_stt()
+                if 3 <= i < PAIRS + 3 and i % 2 == 0:
+                    u = (i - 3) // 2
+                    op_qt(u)
+                    if u % 2 == 1:
+                        ready.extend([(1, u // 2, t, n) for t in range(J) for n in range(2)])
+                if 1 <= i <= len(pieces):
+                    op_stage_q(i - 1)
+                if i >= 4 and i % 4 == 0 and i <= PAIRS:
+                    op_sum(i // 4 - 1)
+                if live:
+                    op_n(i, 0)
+                some_stt()
+                if i >= 5 and i % 4 == 1 and i <= PAIRS + 1:
+                    op_sum_reduce((i - 1) // 4 - 1)
+                if live:
+                    op_n(i, 1)
+                some_stt()
+                if i < len(pieces):
+                    op_stage(i)
+                while ready and len(pending) < MX_BANKS:
+                    emit_mm()
+            while ready or pending:
+                emit_stt()
+                if ready:
+                    emit_mm()

@@ -26,9 +26,11 @@ ACT = mybir.ActivationFunctionType
 ALU = mybir.AluOpType
 AX = mybir.AxisListType
 
-PAIRS = H * B * 2
-Z_ON_GPSIMD = tuple(range(2, 16))
+UNITS = ((0, 0), (0, 1), (1, 0), (1, 1), (2, 0), (3, 0), (2, 1), (3, 1))
+PAIRS = 2 * len(UNITS)
 MX_BANKS = 3
+LAST_F = tuple(u for k, u in enumerate(UNITS) if not any(v[1] == u[1] for v in UNITS[k + 1:]))
+LAST_T = tuple(u for k, u in enumerate(UNITS) if not any(v[0] == u[0] for v in UNITS[k + 1:]))
 
 
 def tile_yatdense_v_kernel(tc, x, weight, alpha, bias, y, x_sq, w_sq, grad_out, out_0, out_1):
@@ -47,6 +49,7 @@ def tile_yatdense_v_kernel(tc, x, weight, alpha, bias, y, x_sq, w_sq, grad_out, 
         psum = ctx.enter_context(tc.psum_pool(name="psum", bufs=1))
 
         ident = keep.tile([P, P], F32, name="ident")
+        junk = keep.tile([P, 1], F32, name="junk")
         wcol = keep.tile([P, H, J], F32, name="wcol")
         xsq = keep.tile([P, B, J], F32, name="xsq")
         xse = keep.tile([P, B, J], F32, name="xse")
@@ -58,7 +61,8 @@ def tile_yatdense_v_kernel(tc, x, weight, alpha, bias, y, x_sq, w_sq, grad_out, 
         acc_f = keep.tile([P, B, J, H], F32, name="acc_f")
         tau = keep.tile([P, B, J], F32, name="tau")
         taus = keep.tile([P, B, J], F32, name="taus")
-        sig = keep.tile([P, H, J], F32, name="sig")
+        sig = keep.tile([P, H, B, J], F32, name="sig")
+        sigt = keep.tile([P, H, J], F32, name="sigt")
         sigs = keep.tile([P, H, J], F32, name="sigs")
         x_raw = keep.tile([P, B, J, D], BF16, name="x_raw")
         w_codes = keep.tile([P, H, D], U32, name="w_codes", align_bytes=64)
@@ -69,43 +73,52 @@ def tile_yatdense_v_kernel(tc, x, weight, alpha, bias, y, x_sq, w_sq, grad_out, 
         f_scales = keep.tile([P, H, B * J * P], U8, name="f_scales", align_bytes=64)
 
         def where(i):
-            h, rest = divmod(i, 4)
-            g, jp = divmod(rest, 2)
-            return h, g, jp
+            h, g = UNITS[i // 2]
+            return h, g, i % 2
 
         yt, gt, zt, qt, rt, mt, nt, dyf, dyt, bk, tcod, wraw, stg = {}, {}, {}, {}, {}, {}, {}, {}, {}, {}, {}, {}, {}
         sums = {}
+        pfs = {}
 
-        def load_pair(i):
+        def load_y(i):
             h, g, jp = where(i)
-            y_tile = io.tile([P, 2, FB], F32, name="y_tile", bufs=4)
-            g_tile = io.tile([P, 2, FB], BF16, name="g_tile", bufs=5)
-            yt[i], gt[i] = y_tile, g_tile
+            y_tile = io.tile([P, 2, FB], F32, name="y_tile", bufs=6)
+            yt[i] = y_tile
             nc.sync.dma_start(out=y_tile[:], in_=y_v[:, g, 2 * jp:2 * jp + 2, h * FB:(h + 1) * FB])
+
+        def load_g(i):
+            h, g, jp = where(i)
+            g_tile = io.tile([P, 2, FB], BF16, name="g_tile", bufs=6)
+            gt[i] = g_tile
             nc.sync.dma_start(out=g_tile[:], in_=g_v[:, g, 2 * jp:2 * jp + 2, h * FB:(h + 1) * FB])
 
         def load_w(h):
-            w_tile = io.tile([P, J, D], BF16, name="w_tile", bufs=4)
+            w_tile = io.tile([P, J, D], BF16, name="w_tile", bufs=3)
             wraw[h] = w_tile
             nc.sync.dma_start(out=w_tile[:], in_=w_v[:, h])
+
+        def load_x(g):
+            nc.sync.dma_start(out=x_raw[:, g], in_=x_v[:, g])
 
         def op_z(i):
             h, g, jp = where(i)
             z_tile = work.tile([P, 2, FB], F32, name="z_tile", bufs=3)
             zt[i] = z_tile
-            eng = nc.gpsimd if i in Z_ON_GPSIMD else nc.vector
+            eng = nc.gpsimd if i in () else nc.vector
             eng.tensor_tensor(out=z_tile[:], in0=yt[i][:], in1=w2b[:, h:h + 1, :].to_broadcast([P, 2, FB]), op=ALU.subtract)
 
         def op_q(i):
             h, g, jp = where(i)
-            q_tile = work.tile([P, 2, FB], F32, name="q_tile", bufs=2)
+            q_tile = work.tile([P, 2, FB], F32, name="q_tile", bufs=3)
             qt[i] = q_tile
             for s in range(2):
                 nc.scalar.activation(
                     out=q_tile[:, s, :].rearrange("p (t m) -> p t m", t=J),
                     in_=zt[i][:, s, :].rearrange("p (m t) -> p t m", t=J),
                     func=ACT.Abs_reciprocal_sqrt, bias=xse[:, g, 2 * jp + s:2 * jp + s + 1], scale=-2.0)
-            nc.scalar.activation(out=q_tile[:], in_=q_tile[:], func=ACT.Square)
+
+        def op_sq(i):
+            nc.scalar.activation(out=qt[i][:], in_=qt[i][:], func=ACT.Square)
 
         def op_r(i):
             r_tile = work.tile([P, 2, FB], F32, name="r_tile", bufs=2)
@@ -126,22 +139,25 @@ def tile_yatdense_v_kernel(tc, x, weight, alpha, bias, y, x_sq, w_sq, grad_out, 
         def op_n(i, s):
             h, g, jp = where(i)
             if s == 0:
-                n_tile = work.tile([P, 2, FB], F32, name="n_tile", bufs=5)
+                n_tile = work.tile([P, 2, FB], F32, name="n_tile", bufs=3)
                 nt[i] = n_tile
             nc.vector.scalar_tensor_tensor(
                 out=nt[i][:, s, :], in0=mt[i][:, s, :], scalar=1.0, in1=rt[i][:, s, :],
                 op0=ALU.mult, op1=ALU.mult, accum_out=acc_f[:, g, 2 * jp + s, h:h + 1])
 
-        def op_fwd(i):
-            f_tile = work.tile([P, 2, P, J], BF16, name="f_tile", bufs=3, align_bytes=64)
-            dyf[i] = f_tile
-            for s in range(2):
-                pf = psum.tile([P, J, P], F32, name="pf", bufs=2)
-                for t in range(J):
-                    cols = slice(t * P, (t + 1) * P)
-                    nc.tensor.matmul(out=pf[:, t, :], lhsT=mt[i][:, s, cols], rhs=ident[:], is_transpose=True, start=True, stop=False)
-                    nc.tensor.matmul(out=pf[:, t, :], lhsT=nt[i][:, s, cols], rhs=ident[:], is_transpose=True, start=False, stop=True)
-                nc.scalar.activation(out=f_tile[:, s], in_=pf[:].rearrange("p t k -> p k t"), func=ACT.Copy, scale=s2[:, 0:1])
+        def op_fwd(i, s):
+            if s == 0:
+                f_tile = work.tile([P, 2, P, J], BF16, name="f_tile", bufs=3, align_bytes=64)
+                dyf[i] = f_tile
+            pf = psum.tile([P, J, P], F32, name="pf", bufs=2)
+            for t in range(J):
+                cols = slice(t * P, (t + 1) * P)
+                nc.tensor.matmul(out=pf[:, t, :], lhsT=mt[i][:, s, cols], rhs=ident[:], is_transpose=True, start=True, stop=False)
+                nc.tensor.matmul(out=pf[:, t, :], lhsT=nt[i][:, s, cols], rhs=ident[:], is_transpose=True, start=False, stop=True)
+            pfs[(i, s)] = pf
+
+        def op_fwd_copy(i, s):
+            nc.scalar.activation(out=dyf[i][:, s], in_=pfs[(i, s)][:].rearrange("p t k -> p k t"), func=ACT.Copy, scale=s2[:, 0:1])
 
         def op_qf(i):
             h, g, jp = where(i)
@@ -162,62 +178,76 @@ def tile_yatdense_v_kernel(tc, x, weight, alpha, bias, y, x_sq, w_sq, grad_out, 
                     j = 2 * jp + s
                     nc.tensor.transpose(bk[i // 2][e][:, j * P:(j + 1) * P], words[:, e:2 * P:2], ident[:])
 
-        def op_back_copy(u):
-            t_tile = work.tile([P, J, P, J], BF16, name="t_tile", bufs=2, align_bytes=64)
-            dyt[u] = t_tile
-            for e in range(2):
-                nc.scalar.copy(out=t_tile[:, 2 * e:2 * e + 2],
-                               in_=bk[u][e][:].bitcast(BF16).rearrange("p (j m i) -> p i m j", j=J, i=2))
+        def op_back_copy(u, e):
+            if e == 0:
+                t_tile = work.tile([P, J, P, J], BF16, name="t_tile", bufs=2, align_bytes=64)
+                dyt[u] = t_tile
+            nc.scalar.copy(out=dyt[u][:, 2 * e:2 * e + 2],
+                           in_=bk[u][e][:].bitcast(BF16).rearrange("p (j m i) -> p i m j", j=J, i=2))
 
         def op_qt(u):
             t_codes = work.tile([P, FB], U32, name="t_codes", bufs=4, align_bytes=64)
             t_scales = work.tile([P, FB], U8, name="t_scales", bufs=4, align_bytes=64)
-            tcod[u] = (t_codes, t_scales)
+            tcod[UNITS[u]] = (t_codes, t_scales)
             nc.vector.quantize_mx(out=t_codes[:].bitcast(E5M2), scales=t_scales[:], in_=dyt[u][:].rearrange("p t m j -> p (t m j)"))
 
-        def op_sum(h):
+        def op_sum(u):
             ps = psum.tile([P, J, P], F32, name="ps", bufs=1)
-            sums[h] = ps
+            sums[u] = ps
             for t in range(J):
-                for k in range(8):
-                    i, s = 4 * h + k // 2, k % 2
-                    nc.tensor.matmul(out=ps[:, t, :], lhsT=nt[i][:, s, t * P:(t + 1) * P], rhs=ident[:], is_transpose=True, start=(k == 0), stop=(k == 7))
+                for k in range(4):
+                    i, s = 2 * u + k // 2, k % 2
+                    nc.tensor.matmul(out=ps[:, t, :], lhsT=nt[i][:, s, t * P:(t + 1) * P], rhs=ident[:], is_transpose=True, start=(k == 0), stop=(k == 3))
 
-        def op_sum_reduce(h):
-            nc.vector.tensor_reduce(out=sig[:, h, :], in_=sums[h][:], axis=AX.X, op=ALU.add)
-            nc.vector.tensor_scalar(out=sigs[:, h, :], in0=sig[:, h, :], scalar1=ns2[:, 0:1], scalar2=None, op0=ALU.mult)
+        def op_sum_reduce(u):
+            h, g = UNITS[u]
+            nc.vector.tensor_reduce(out=sig[:, h, g, :], in_=sums[u][:], axis=AX.X, op=ALU.add)
+
+        def op_sig(h):
+            nc.vector.tensor_tensor(out=sigt[:, h, :], in0=sig[:, h, 0, :], in1=sig[:, h, 1, :], op=ALU.add)
+            nc.vector.tensor_scalar(out=sigs[:, h, :], in0=sigt[:, h, :], scalar1=ns2[:, 0:1], scalar2=None, op0=ALU.mult)
 
         def op_tau(i):
             h, g, jp = where(i)
             nc.vector.tensor_reduce(out=tau[:, g, 2 * jp:2 * jp + 2], in_=acc_f[:, g, 2 * jp:2 * jp + 2, :], axis=AX.X, op=ALU.add)
             nc.vector.tensor_scalar(out=taus[:, g, 2 * jp:2 * jp + 2], in0=tau[:, g, 2 * jp:2 * jp + 2], scalar1=ns2[:, 0:1], scalar2=None, op0=ALU.mult)
 
-        pieces = [("x", g, n) for g in range(B) for n in range(2)] + [("w", h, n) for h in range(H) for n in range(2)]
+        SW = 256
+        pieces = [("x", g, n) for g in range(B) for n in range(D // SW)] + [("w", h, n) for h in range(H) for n in range(D // SW)]
 
-        def op_stage(k):
+        def op_stage(k, eng):
             kind, a, n = pieces[k]
-            s_tile = work.tile([P, NT, J], BF16, name="s_tile", bufs=2, align_bytes=64)
+            s_tile = work.tile([P, SW, J], BF16, name="s_tile", bufs=4, align_bytes=64)
             stg[k] = s_tile
-            src = x_raw[:, a, :, n * NT:(n + 1) * NT] if kind == "x" else wraw[a][:, :, n * NT:(n + 1) * NT]
-            nc.scalar.copy(out=s_tile[:], in_=src.rearrange("p j d -> p d j"))
+            src = x_raw[:, a, :, n * SW:(n + 1) * SW] if kind == "x" else wraw[a][:, :, n * SW:(n + 1) * SW]
+            if eng == "v":
+                nc.vector.tensor_copy(out=s_tile[:], in_=src.rearrange("p j d -> p d j"))
+            else:
+                nc.scalar.copy(out=s_tile[:], in_=src.rearrange("p j d -> p d j"))
 
         def op_stage_q(k):
             kind, a, n = pieces[k]
             codes, scales = (x_codes, x_scales) if kind == "x" else (w_codes, w_scales)
-            nc.vector.quantize_mx(out=codes[:, a, n * NT:(n + 1) * NT].bitcast(E4M3), scales=scales[:, a, n * NT:(n + 1) * NT],
+            nc.vector.quantize_mx(out=codes[:, a, n * SW:(n + 1) * SW].bitcast(E4M3), scales=scales[:, a, n * SW:(n + 1) * SW],
                                   in_=stg[k][:].rearrange("p d j -> p (d j)"))
 
         ready = []
         pending = []
         outs = {}
+        tail = []
+        nbufs = {"acc": MX_BANKS, "pf": 2, "b0": 1, "b1": 1, "ps": 1}
 
         def emit_mm():
             kind, a, b, n = ready.pop(0)
-            acc = psum.tile([P, NT], F32, name="acc", bufs=MX_BANKS)
+            tag = "acc"
+            if tail:
+                tag = tail.pop(0)
+                tail.append(tag)
+            acc = psum.tile([P, NT], F32, name=tag, bufs=nbufs[tag])
             cols = slice(n * NT, (n + 1) * NT)
             if kind == 1:
                 for g in range(B):
-                    codes, scales = tcod[2 * a + g]
+                    codes, scales = tcod[(a, g)]
                     nc.tensor.matmul_mx(out=acc[:], lhsT=codes[:, b * P:(b + 1) * P].bitcast(E5M2), lhsT_scale=scales[:, b * P:(b + 1) * P],
                                         rhs=x_codes[:, g, cols].bitcast(E4M3), rhs_scale=x_scales[:, g, cols], start=(g == 0), stop=(g == B - 1))
             else:
@@ -231,7 +261,7 @@ def tile_yatdense_v_kernel(tc, x, weight, alpha, bias, y, x_sq, w_sq, grad_out, 
             kind, a, b, n, acc = pending.pop(0)
             cols = slice(n * NT, (n + 1) * NT)
             if n == 0:
-                o_tile = io.tile([P, D], F32, name="o_tile", bufs=3)
+                o_tile = io.tile([P, D], F32, name="o_tile", bufs=4)
                 outs[(kind, a, b)] = o_tile
             o = outs[(kind, a, b)]
             if kind == 1:
@@ -250,73 +280,118 @@ def tile_yatdense_v_kernel(tc, x, weight, alpha, bias, y, x_sq, w_sq, grad_out, 
             nc.sync.dma_start(out=wcol[:], in_=w_sq.rearrange("(h m t) -> m h t", h=H, t=J))
             nc.sync.dma_start(out=xsq[:], in_=x_sq.rearrange("g (p j) o -> p g (j o)", j=J))
             nc.sync.dma_start(out=al[:], in_=alpha.partition_broadcast(P))
+            load_y(0)
             make_identity(nc, ident[:])
-            load_pair(0)
-            load_pair(1)
-            nc.scalar.activation(out=sc[:], in_=al[:], func=ACT.Exp, scale=LOG_BASE)
-            nc.vector.tensor_scalar(out=xse[:], in0=xsq[:], scalar1=EPS, scalar2=None, op0=ALU.add)
-            for h in range(H):
+            nc.vector.memset(junk[:], 1.0)
+            nc.scalar.activation(out=junk[:], in_=junk[:], func=ACT.Exp)
+            load_g(0)
+            load_y(1)
+            load_g(1)
+
+            def spread(h, eng):
                 pw = psum.tile([P, J, P], F32, name="pf", bufs=2)
                 for t in range(J):
                     nc.tensor.transpose(pw[:, t, :], wcol[:, h, t:t + 1].to_broadcast([P, P]), ident[:])
-                nc.scalar.activation(out=w2b[:, h, :].rearrange("p (m t) -> p m t", t=J), in_=pw[:].rearrange("p t m -> p m t"), func=ACT.Copy, scale=0.5)
-            nc.vector.tensor_scalar(out=s2[:], in0=sc[:], scalar1=2.0, scalar2=None, op0=ALU.mult)
-            nc.vector.tensor_scalar(out=ns2[:], in0=sc[:], scalar1=-2.0, scalar2=None, op0=ALU.mult)
-            nc.sync.dma_start(out=x_raw[:, 0], in_=x_v[:, 0])
-            load_pair(2)
-            nc.sync.dma_start(out=x_raw[:, 1], in_=x_v[:, 1])
-            load_pair(3)
-            op_z(0)
-            op_z(1)
-            op_q(0)
-            last = PAIRS + 3
-            for i in range(last):
+                dst, srcp = w2b[:, h, :].rearrange("p (m t) -> p m t", t=J), pw[:].rearrange("p t m -> p m t")
+                if eng == "v":
+                    nc.vector.tensor_scalar(out=dst, in0=srcp, scalar1=0.5, scalar2=None, op0=ALU.mult)
+                else:
+                    nc.scalar.activation(out=dst, in_=srcp, func=ACT.Copy, scale=0.5)
+
+            nc.scalar.activation(out=sc[:], in_=al[:], func=ACT.Exp, scale=LOG_BASE)
+            nc.scalar.activation(out=junk[:], in_=junk[:], func=ACT.Abs_reciprocal_sqrt)
+            nc.vector.tensor_scalar(out=xse[:], in0=xsq[:], scalar1=EPS, scalar2=None, op0=ALU.add)
+            spread(0, "v")
+            load_y(2)
+            load_g(2)
+            load_x(0)
+            nloaded = 3
+            QL, ZL = 2, 3
+            for k in range(ZL):
+                op_z(k)
+                if k == 0:
+                    spread(1, "v")
+                    nc.vector.tensor_scalar(out=s2[:], in0=sc[:], scalar1=2.0, scalar2=None, op0=ALU.mult)
+                    nc.vector.tensor_scalar(out=ns2[:], in0=sc[:], scalar1=-2.0, scalar2=None, op0=ALU.mult)
+            for k in range(QL):
+                op_q(k)
+                op_sq(k)
+            spread(2, "v")
+            spread(3, "v")
+            nstage = 0
+            nquant = 0
+            nw = 0
+            for i in range(PAIRS + 3):
                 live = i < PAIRS
-                if 1 <= i and i + 3 < PAIRS:
-                    load_pair(i + 3)
-                if 1 <= i <= 4:
-                    load_w(i - 1)
-                if i + 1 < PAIRS:
-                    op_q(i + 1)
+                while nloaded < min(PAIRS, i + 5):
+                    load_y(nloaded)
+                    load_g(nloaded)
+                    nloaded += 1
+                if i == 0:
+                    load_x(1)
+                while nw < H and i >= (0, 2, 4, 7)[nw]:
+                    load_w(nw)
+                    nw += 1
+                prev = 1 <= i < PAIRS + 1
+                if prev:
+                    op_fwd(i - 1, 0)
+                    op_fwd(i - 1, 1)
                 if live:
                     op_r(i)
-                if 2 <= i < PAIRS + 2:
-                    op_back(i - 2)
-                if 1 <= i < PAIRS + 1:
-                    op_fwd(i - 1)
+                if i + QL < PAIRS:
+                    op_q(i + QL)
+                if prev:
+                    op_fwd_copy(i - 1, 0)
+                    op_fwd_copy(i - 1, 1)
+                    op_back(i - 1)
+                    if i % 2 == 0:
+                        op_sum((i - 1) // 2)
+                if i + QL < PAIRS:
+                    op_sq(i + QL)
+                if i + ZL < PAIRS:
+                    op_z(i + ZL)
+                some_stt()
+                if live:
+                    op_m(i)
                 if 2 <= i < PAIRS + 2:
                     op_qf(i - 2)
-                    if i - 2 >= PAIRS - 4:
+                    if UNITS[(i - 2) // 2] in LAST_F:
                         op_tau(i - 2)
                         h, g, jp = where(i - 2)
                         ready.extend([(0, g, 2 * jp + s, n) for s in range(2) for n in range(2)])
-                if i + 2 < PAIRS:
-                    op_z(i + 2)
-                if live:
-                    op_m(i)
-                if 2 <= i < PAIRS + 2 and i % 2 == 1:
-                    op_back_copy((i - 2) // 2)
                 some_stt()
-                if 3 <= i < PAIRS + 3 and i % 2 == 0:
+                if 3 <= i < PAIRS + 3 and i % 2 == 1:
                     u = (i - 3) // 2
                     op_qt(u)
-                    if u % 2 == 1:
-                        ready.extend([(1, u // 2, t, n) for t in range(J) for n in range(2)])
-                if 1 <= i <= len(pieces):
-                    op_stage_q(i - 1)
-                if i >= 4 and i % 4 == 0 and i <= PAIRS:
-                    op_sum(i // 4 - 1)
+                    if UNITS[u] in LAST_T:
+                        ready.extend([(1, UNITS[u][0], t, n) for t in range(J) for n in range(2)])
+                for k in range((0, 0, 0, 0, 0, 0, 0, 0, 0, 0, 0, 0, 0, 0, 0, 0)[min(i, 15)]):
+                    op_stage(nstage, "v")
+                    nstage += 1
                 if live:
                     op_n(i, 0)
                 some_stt()
-                if i >= 5 and i % 4 == 1 and i <= PAIRS + 1:
-                    op_sum_reduce((i - 1) // 4 - 1)
+                if i >= 3 and i % 2 == 1 and i <= PAIRS + 1:
+                    u = (i - 3) // 2
+                    op_sum_reduce(u)
+                    if UNITS[u] in LAST_T:
+                        op_sig(UNITS[u][0])
                 if live:
                     op_n(i, 1)
+                while nquant < nstage - (1, 1, 1, 1, 1, 1, 1, 1, 1, 1, 1, 0, 0, 0, 0, 0)[min(i, 15)]:
+                    op_stage_q(nquant)
+                    nquant += 1
                 some_stt()
-                if i < len(pieces):
-                    op_stage(i)
-                while ready and len(pending) < MX_BANKS:
+                if prev and i % 2 == 0:
+                    op_back_copy((i - 1) // 2, 0)
+                    op_back_copy((i - 1) // 2, 1)
+                for k in range((2, 2, 2, 2, 2, 2, 2, 2, 2, 2, 2, 2, 0, 0, 0, 0)[min(i, 15)]):
+                    if nstage < len(pieces):
+                        op_stage(nstage, "s")
+                        nstage += 1
+                if i >= PAIRS + 1 and not tail:
+                    tail.extend(["acc", "pf", "acc", "b0", "acc", "b1", "pf", "ps"])
+                while ready and len(pending) < (MX_BANKS if not tail else 7):
                     emit_mm()
             while ready or pending:
                 emit_stt()

@@ -109,40 +109,40 @@ def tile_yatdense_v_kernel(tc, x, weight, alpha, bias, y, x_sq, w_sq, grad_out, 
 
         def op_q(i):
             h, g, jp = where(i)
-            q_tile = work.tile([P, 2, FB], F32, name="q_tile", bufs=3)
+            q_tile = work.tile([P, J, 2, P], F32, name="q_tile", bufs=3)
             qt[i] = q_tile
             for s in range(2):
                 nc.scalar.activation(
-                    out=q_tile[:, s, :].rearrange("p (t m) -> p t m", t=J),
-                    in_=zt[i][:, s, :].rearrange("p (m t) -> p t m", t=J),
+                    out=q_tile[:, :, s, :].rearrange("p t (a b) -> p a t b", b=4),
+                    in_=zt[i][:, s, :].rearrange("p (a b t) -> p a t b", b=4, t=J),
                     func=ACT.Abs_reciprocal_sqrt, bias=xse[:, g, 2 * jp + s:2 * jp + s + 1], scale=-2.0)
 
         def op_sq(i):
             nc.scalar.activation(out=qt[i][:], in_=qt[i][:], func=ACT.Square)
 
         def op_r(i):
-            r_tile = work.tile([P, 2, FB], F32, name="r_tile", bufs=2)
+            r_tile = work.tile([P, J, 2, P], F32, name="r_tile", bufs=2)
             rt[i] = r_tile
             nc.vector.tensor_tensor(
-                out=r_tile[:].rearrange("p s (t m) -> p s t m", t=J),
-                in0=yt[i][:].rearrange("p s (m t) -> p s t m", t=J),
-                in1=qt[i][:].rearrange("p s (t m) -> p s t m", t=J), op=ALU.mult)
+                out=r_tile[:].rearrange("p t s (a b) -> p (s a) t b", b=4),
+                in0=yt[i][:].rearrange("p s (a b t) -> p (s a) t b", b=4, t=J),
+                in1=qt[i][:].rearrange("p t s (a b) -> p (s a) t b", b=4), op=ALU.mult)
 
         def op_m(i):
-            m_tile = work.tile([P, 2, FB], F32, name="m_tile", bufs=2)
+            m_tile = work.tile([P, J, 2, P], F32, name="m_tile", bufs=2)
             mt[i] = m_tile
             nc.vector.tensor_tensor(
-                out=m_tile[:].rearrange("p s (t m) -> p s t m", t=J),
-                in0=rt[i][:].rearrange("p s (t m) -> p s t m", t=J),
-                in1=gt[i][:].rearrange("p s (m t) -> p s t m", t=J), op=ALU.mult)
+                out=m_tile[:].rearrange("p t s (a b) -> p (s a) t b", b=4),
+                in0=rt[i][:].rearrange("p t s (a b) -> p (s a) t b", b=4),
+                in1=gt[i][:].rearrange("p s (a b t) -> p (s a) t b", b=4, t=J), op=ALU.mult)
 
         def op_n(i, s):
             h, g, jp = where(i)
             if s == 0:
-                n_tile = work.tile([P, 2, FB], F32, name="n_tile", bufs=3)
+                n_tile = work.tile([P, J, 2, P], F32, name="n_tile", bufs=3)
                 nt[i] = n_tile
             nc.vector.scalar_tensor_tensor(
-                out=nt[i][:, s, :], in0=mt[i][:, s, :], scalar=1.0, in1=rt[i][:, s, :],
+                out=nt[i][:, :, s, :], in0=mt[i][:, :, s, :], scalar=1.0, in1=rt[i][:, :, s, :],
                 op0=ALU.mult, op1=ALU.mult, accum_out=acc_f[:, g, 2 * jp + s, h:h + 1])
 
         def op_fwd(i, s):
@@ -151,9 +151,8 @@ def tile_yatdense_v_kernel(tc, x, weight, alpha, bias, y, x_sq, w_sq, grad_out, 
                 dyf[i] = f_tile
             pf = psum.tile([P, J, P], F32, name="pf", bufs=2)
             for t in range(J):
-                cols = slice(t * P, (t + 1) * P)
-                nc.tensor.matmul(out=pf[:, t, :], lhsT=mt[i][:, s, cols], rhs=ident[:], is_transpose=True, start=True, stop=False)
-                nc.tensor.matmul(out=pf[:, t, :], lhsT=nt[i][:, s, cols], rhs=ident[:], is_transpose=True, start=False, stop=True)
+                nc.tensor.matmul(out=pf[:, t, :], lhsT=mt[i][:, t, s, :], rhs=ident[:], is_transpose=True, start=True, stop=False)
+                nc.tensor.matmul(out=pf[:, t, :], lhsT=nt[i][:, t, s, :], rhs=ident[:], is_transpose=True, start=False, stop=True)
             pfs[(i, s)] = pf
 
         def op_fwd_copy(i, s):
@@ -197,7 +196,7 @@ def tile_yatdense_v_kernel(tc, x, weight, alpha, bias, y, x_sq, w_sq, grad_out, 
             for t in range(J):
                 for k in range(4):
                     i, s = 2 * u + k // 2, k % 2
-                    nc.tensor.matmul(out=ps[:, t, :], lhsT=nt[i][:, s, t * P:(t + 1) * P], rhs=ident[:], is_transpose=True, start=(k == 0), stop=(k == 3))
+                    nc.tensor.matmul(out=ps[:, t, :], lhsT=nt[i][:, t, s, :], rhs=ident[:], is_transpose=True, start=(k == 0), stop=(k == 3))
 
         def op_sum_reduce(u):
             h, g = UNITS[u]
@@ -221,9 +220,9 @@ def tile_yatdense_v_kernel(tc, x, weight, alpha, bias, y, x_sq, w_sq, grad_out, 
             stg[k] = s_tile
             src = x_raw[:, a, :, n * SW:(n + 1) * SW] if kind == "x" else wraw[a][:, :, n * SW:(n + 1) * SW]
             if eng == "v":
-                nc.vector.tensor_copy(out=s_tile[:], in_=src.rearrange("p j d -> p d j"))
+                nc.vector.tensor_copy(out=s_tile[:].rearrange("p (c i) j -> p c j i", i=4), in_=src.rearrange("p j (c i) -> p c j i", i=4))
             else:
-                nc.scalar.copy(out=s_tile[:], in_=src.rearrange("p j d -> p d j"))
+                nc.scalar.copy(out=s_tile[:].rearrange("p (c i) j -> p c j i", i=4), in_=src.rearrange("p j (c i) -> p c j i", i=4))
 
         def op_stage_q(k):
             kind, a, n = pieces[k]

@@ -31,6 +31,7 @@ PAIRS = 2 * len(UNITS)
 MX_BANKS = 3
 LAST_F = tuple(u for k, u in enumerate(UNITS) if not any(v[1] == u[1] for v in UNITS[k + 1:]))
 LAST_T = tuple(u for k, u in enumerate(UNITS) if not any(v[0] == u[0] for v in UNITS[k + 1:]))
+ONES = 64
 
 
 def tile_yatdense_v_kernel(tc, x, weight, alpha, bias, y, x_sq, w_sq, grad_out, out_0, out_1):
@@ -62,7 +63,7 @@ def tile_yatdense_v_kernel(tc, x, weight, alpha, bias, y, x_sq, w_sq, grad_out, 
         tau = keep.tile([P, B, J], F32, name="tau")
         taus = keep.tile([P, B, J], F32, name="taus")
         sig = keep.tile([P, H, B, J], F32, name="sig")
-        sigt = keep.tile([P, H, J], F32, name="sigt")
+        ones = keep.tile([P, ONES], F32, name="ones")
         sigs = keep.tile([P, H, J], F32, name="sigs")
         x_raw = keep.tile([P, B, J, D], BF16, name="x_raw")
         w_codes = keep.tile([P, H, D], U32, name="w_codes", align_bytes=64)
@@ -102,19 +103,18 @@ def tile_yatdense_v_kernel(tc, x, weight, alpha, bias, y, x_sq, w_sq, grad_out, 
 
         def op_z(i):
             h, g, jp = where(i)
-            z_tile = work.tile([P, 2, FB], F32, name="z_tile", bufs=3)
+            z_tile = work.tile([P, 2, FB], F32, name="z_tile", bufs=2)
             zt[i] = z_tile
             eng = nc.gpsimd if i in () else nc.vector
             eng.tensor_tensor(out=z_tile[:], in0=yt[i][:], in1=w2b[:, h:h + 1, :].to_broadcast([P, 2, FB]), op=ALU.subtract)
 
         def op_q(i):
             h, g, jp = where(i)
-            q_tile = work.tile([P, J, 2, P], F32, name="q_tile", bufs=3)
+            q_tile = work.tile([P, 2, FB], F32, name="q_tile", bufs=3)
             qt[i] = q_tile
             for s in range(2):
                 nc.scalar.activation(
-                    out=q_tile[:, :, s, :].rearrange("p t (a b) -> p a t b", b=4),
-                    in_=zt[i][:, s, :].rearrange("p (a b t) -> p a t b", b=4, t=J),
+                    out=q_tile[:, s, :], in_=zt[i][:, s, :],
                     func=ACT.Abs_reciprocal_sqrt, bias=xse[:, g, 2 * jp + s:2 * jp + s + 1], scale=-2.0)
 
         def op_sq(i):
@@ -124,9 +124,9 @@ def tile_yatdense_v_kernel(tc, x, weight, alpha, bias, y, x_sq, w_sq, grad_out, 
             r_tile = work.tile([P, J, 2, P], F32, name="r_tile", bufs=2)
             rt[i] = r_tile
             nc.vector.tensor_tensor(
-                out=r_tile[:].rearrange("p t s (a b) -> p (s a) t b", b=4),
-                in0=yt[i][:].rearrange("p s (a b t) -> p (s a) t b", b=4, t=J),
-                in1=qt[i][:].rearrange("p t s (a b) -> p (s a) t b", b=4), op=ALU.mult)
+                out=r_tile[:].rearrange("p t s m -> p (s m) t"),
+                in0=yt[i][:].rearrange("p s (m t) -> p (s m) t", t=J),
+                in1=qt[i][:].rearrange("p s (m t) -> p (s m) t", t=J), op=ALU.mult)
 
         def op_m(i):
             m_tile = work.tile([P, J, 2, P], F32, name="m_tile", bufs=2)
@@ -139,7 +139,7 @@ def tile_yatdense_v_kernel(tc, x, weight, alpha, bias, y, x_sq, w_sq, grad_out, 
         def op_n(i, s):
             h, g, jp = where(i)
             if s == 0:
-                n_tile = work.tile([P, J, 2, P], F32, name="n_tile", bufs=3)
+                n_tile = work.tile([P, J, 2, P], F32, name="n_tile", bufs=4)
                 nt[i] = n_tile
             nc.vector.scalar_tensor_tensor(
                 out=nt[i][:, :, s, :], in0=mt[i][:, :, s, :], scalar=1.0, in1=rt[i][:, :, s, :],
@@ -190,21 +190,20 @@ def tile_yatdense_v_kernel(tc, x, weight, alpha, bias, y, x_sq, w_sq, grad_out, 
             tcod[UNITS[u]] = (t_codes, t_scales)
             nc.vector.quantize_mx(out=t_codes[:].bitcast(E5M2), scales=t_scales[:], in_=dyt[u][:].rearrange("p t m j -> p (t m j)"))
 
-        def op_sum(u):
-            ps = psum.tile([P, J, P], F32, name="ps", bufs=1)
-            sums[u] = ps
-            for t in range(J):
-                for k in range(4):
-                    i, s = 2 * u + k // 2, k % 2
-                    nc.tensor.matmul(out=ps[:, t, :], lhsT=nt[i][:, t, s, :], rhs=ident[:], is_transpose=True, start=(k == 0), stop=(k == 3))
+        def op_sum(u, t):
+            if t == 0:
+                ps = psum.tile([P, J, ONES], F32, name="ps", bufs=1)
+                sums[u] = ps
+            for k in range(4):
+                i, s = 2 * u + k // 2, k % 2
+                nc.tensor.matmul(out=sums[u][:, t, :], lhsT=nt[i][:, t, s, :], rhs=ones[:], start=(k == 0), stop=(k == 3))
 
-        def op_sum_reduce(u):
+        def op_sum_scale(u):
             h, g = UNITS[u]
-            nc.vector.tensor_reduce(out=sig[:, h, g, :], in_=sums[u][:], axis=AX.X, op=ALU.add)
+            nc.vector.tensor_scalar(out=sig[:, h, g, :], in0=sums[u][:, :, 0:1].rearrange("p t o -> p (t o)"), scalar1=ns2[:, 0:1], scalar2=None, op0=ALU.mult)
 
         def op_sig(h):
-            nc.vector.tensor_tensor(out=sigt[:, h, :], in0=sig[:, h, 0, :], in1=sig[:, h, 1, :], op=ALU.add)
-            nc.vector.tensor_scalar(out=sigs[:, h, :], in0=sigt[:, h, :], scalar1=ns2[:, 0:1], scalar2=None, op0=ALU.mult)
+            nc.vector.tensor_tensor(out=sigs[:, h, :], in0=sig[:, h, 0, :], in1=sig[:, h, 1, :], op=ALU.add)
 
         def op_tau(i):
             h, g, jp = where(i)
@@ -282,10 +281,10 @@ def tile_yatdense_v_kernel(tc, x, weight, alpha, bias, y, x_sq, w_sq, grad_out, 
             load_y(0)
             make_identity(nc, ident[:])
             nc.vector.memset(junk[:], 1.0)
+            nc.vector.memset(ones[:], 1.0)
             nc.scalar.activation(out=junk[:], in_=junk[:], func=ACT.Exp)
-            load_g(0)
             load_y(1)
-            load_g(1)
+            load_g(0)
 
             def spread(h, eng):
                 pw = psum.tile([P, J, P], F32, name="pf", bufs=2)
@@ -302,11 +301,14 @@ def tile_yatdense_v_kernel(tc, x, weight, alpha, bias, y, x_sq, w_sq, grad_out, 
             nc.vector.tensor_scalar(out=xse[:], in0=xsq[:], scalar1=EPS, scalar2=None, op0=ALU.add)
             spread(0, "v")
             load_y(2)
+            load_g(1)
+            load_y(3)
             load_g(2)
+            load_g(3)
             load_x(0)
-            nloaded = 3
+            nloaded = 4
             QL, ZL = 2, 3
-            for k in range(ZL):
+            for k in range(QL):
                 op_z(k)
                 if k == 0:
                     spread(1, "v")
@@ -317,10 +319,22 @@ def tile_yatdense_v_kernel(tc, x, weight, alpha, bias, y, x_sq, w_sq, grad_out, 
                 op_sq(k)
             spread(2, "v")
             spread(3, "v")
+            def feature_side(i):
+                op_qf(i)
+                if UNITS[i // 2] in LAST_F:
+                    op_tau(i)
+                    h, g, jp = where(i)
+                    ready.extend([(0, g, 2 * jp + s, n) for s in range(2) for n in range(2)])
+
+            def pump():
+                some_stt()
+                if ready and len(pending) < MX_BANKS:
+                    emit_mm()
+
             nstage = 0
             nquant = 0
             nw = 0
-            for i in range(PAIRS + 3):
+            for i in range(PAIRS + 2):
                 live = i < PAIRS
                 while nloaded < min(PAIRS, i + 5):
                     load_y(nloaded)
@@ -337,31 +351,40 @@ def tile_yatdense_v_kernel(tc, x, weight, alpha, bias, y, x_sq, w_sq, grad_out, 
                     op_fwd(i - 1, 1)
                 if live:
                     op_r(i)
+                if i == 0:
+                    for k in range(QL, ZL):
+                        op_z(k)
                 if i + QL < PAIRS:
                     op_q(i + QL)
+                if 2 <= i < PAIRS + 2:
+                    op_sum((i - 2) // 2, 2 * (i % 2))
+                    if i % 2 == 1:
+                        op_sum((i - 2) // 2, 3)
                 if prev:
                     op_fwd_copy(i - 1, 0)
                     op_fwd_copy(i - 1, 1)
                     op_back(i - 1)
-                    if i % 2 == 0:
-                        op_sum((i - 1) // 2)
+                if 2 <= i < PAIRS + 2 and i % 2 == 0:
+                    op_sum((i - 2) // 2, 1)
                 if i + QL < PAIRS:
                     op_sq(i + QL)
                 if i + ZL < PAIRS:
                     op_z(i + ZL)
-                some_stt()
                 if live:
                     op_m(i)
-                if 2 <= i < PAIRS + 2:
-                    op_qf(i - 2)
-                    if UNITS[(i - 2) // 2] in LAST_F:
-                        op_tau(i - 2)
-                        h, g, jp = where(i - 2)
-                        ready.extend([(0, g, 2 * jp + s, n) for s in range(2) for n in range(2)])
-                some_stt()
+                pump()
+                while nquant < nstage - (1, 1, 1, 1, 1, 1, 1, 1, 1, 1, 1, 1, 0, 0, 0, 0)[min(i, 15)]:
+                    op_stage_q(nquant)
+                    nquant += 1
+                if 2 <= i < PAIRS:
+                    feature_side(i - 2)
+                pump()
                 if 3 <= i < PAIRS + 3 and i % 2 == 1:
                     u = (i - 3) // 2
                     op_qt(u)
+                    op_sum_scale(u)
+                    if UNITS[u] in LAST_T:
+                        op_sig(UNITS[u][0])
                     if UNITS[u] in LAST_T:
                         ready.extend([(1, UNITS[u][0], t, n) for t in range(J) for n in range(2)])
                 for k in range((0, 0, 0, 0, 0, 0, 0, 0, 0, 0, 0, 0, 0, 0, 0, 0)[min(i, 15)]):
@@ -369,18 +392,12 @@ def tile_yatdense_v_kernel(tc, x, weight, alpha, bias, y, x_sq, w_sq, grad_out, 
                     nstage += 1
                 if live:
                     op_n(i, 0)
-                some_stt()
-                if i >= 3 and i % 2 == 1 and i <= PAIRS + 1:
-                    u = (i - 3) // 2
-                    op_sum_reduce(u)
-                    if UNITS[u] in LAST_T:
-                        op_sig(UNITS[u][0])
+                pump()
                 if live:
                     op_n(i, 1)
-                while nquant < nstage - (1, 1, 1, 1, 1, 1, 1, 1, 1, 1, 1, 0, 0, 0, 0, 0)[min(i, 15)]:
-                    op_stage_q(nquant)
-                    nquant += 1
-                some_stt()
+                pump()
+                if i >= PAIRS - 1 and prev:
+                    feature_side(i - 1)
                 if prev and i % 2 == 0:
                     op_back_copy((i - 1) // 2, 0)
                     op_back_copy((i - 1) // 2, 1)
@@ -392,6 +409,10 @@ def tile_yatdense_v_kernel(tc, x, weight, alpha, bias, y, x_sq, w_sq, grad_out, 
                     tail.extend(["acc", "pf", "acc", "b0", "acc", "b1", "pf", "ps"])
                 while ready and len(pending) < (MX_BANKS if not tail else 7):
                     emit_mm()
+                for k in range((0, 0, 0, 0, 0, 0, 0, 0, 0, 0, 0, 0, 0, 1, 2, 0, 0, 0, 0)[i] if i < len((0, 0, 0, 0, 0, 0, 0, 0, 0, 0, 0, 0, 0, 1, 2, 0, 0, 0, 0)) else 0):
+                    pump()
+                    if ready:
+                        emit_mm()
             while ready or pending:
                 emit_stt()
                 if ready:

@@ -6,13 +6,13 @@ from concourse.masks import make_identity
 
 B, S, D, F = 2, 512, 1024, 2048
 FLOPS = 2 * 2 * B * S * D * F
-BYTES = 2 * B * S * D + 2 * F * D + 2 * B * S * F + 4 * B * S * F + 4 * (B * S + F) + 2 + 4 * B * S * D + 4 * F * D
+BYTES = 2 * (B * S * D + F * D + B * S * F) + 4 * (B * S * F + B * S + F) + 2 + 4 * (B * S * D + F * D)
 
 P = 128
 J = 4
-H = 4
-FB = 512
-NT = 512
+K = P * J
+H = F // K
+N = 512
 EPS = 1e-6
 LOG_BASE = math.log(math.sqrt(F) / math.log(1.0 + F))
 
@@ -26,394 +26,403 @@ ACT = mybir.ActivationFunctionType
 ALU = mybir.AluOpType
 AX = mybir.AxisListType
 
-UNITS = ((0, 0), (0, 1), (1, 0), (1, 1), (2, 0), (3, 0), (2, 1), (3, 1))
-PAIRS = 2 * len(UNITS)
-MX_BANKS = 3
-LAST_F = tuple(u for k, u in enumerate(UNITS) if not any(v[1] == u[1] for v in UNITS[k + 1:]))
-LAST_T = tuple(u for k, u in enumerate(UNITS) if not any(v[0] == u[0] for v in UNITS[k + 1:]))
+UNITS = tuple((b, h) for b in range(B) for h in range(H))
+STEPS = 2 * len(UNITS)
+
+PIECE = 256
+SCALAR_PIECES = (1, 1, 1, 1, 1, 2, 2, 2, 2, 3, 3, 0, 0, 0, 0, 0)
+VECTOR_STEPS = range(1, 6)
+WEIGHT_NEEDED = 2 * H
+X_NEEDED = 2 * H + 3
+
+ACC_BANKS = 3
+READ_LAG = 4
 ONES = 64
 
 
 def tile_yatdense_v_kernel(tc, x, weight, alpha, bias, y, x_sq, w_sq, grad_out, out_0, out_1):
     nc = tc.nc
-    x_v = x.rearrange("g (p j) d -> p g j d", j=J)
-    w_v = weight.rearrange("(h p j) d -> p h j d", h=H, j=J)
-    y_v = y.rearrange("g (p j) f -> p g j f", j=J)
-    g_v = grad_out.rearrange("g (p j) f -> p g j f", j=J)
-    o0_v = out_0.rearrange("g (p j) d -> p g j d", j=J)
-    o1_v = out_1.rearrange("(h p j) d -> p h j d", h=H, j=J)
+    x_v = x.rearrange("b (p j) d -> p b j d", j=J)
+    weight_v = weight.rearrange("(h m t) d -> m h t d", h=H, t=J)
+    y_v = y.rearrange("b (p j) f -> p b j f", j=J)
+    grad_v = grad_out.rearrange("b (p j) f -> p b j f", j=J)
+    out_0_v = out_0.rearrange("b (p j) d -> p b j d", j=J)
+    out_1_v = out_1.rearrange("(h m t) d -> m h t d", h=H, t=J)
 
     with ExitStack() as ctx:
         keep = ctx.enter_context(tc.tile_pool(name="keep", bufs=1))
-        io = ctx.enter_context(tc.tile_pool(name="io", bufs=4))
+        io = ctx.enter_context(tc.tile_pool(name="io", bufs=5))
         work = ctx.enter_context(tc.tile_pool(name="work", bufs=2))
         psum = ctx.enter_context(tc.psum_pool(name="psum", bufs=1))
 
         ident = keep.tile([P, P], F32, name="ident")
-        junk = keep.tile([P, 1], F32, name="junk")
-        wcol = keep.tile([P, H, J], F32, name="wcol")
-        xsq = keep.tile([P, B, J], F32, name="xsq")
-        xse = keep.tile([P, B, J], F32, name="xse")
-        al = keep.tile([P, 1], BF16, name="al")
-        sc = keep.tile([P, 1], F32, name="sc")
-        s2 = keep.tile([P, 1], F32, name="s2")
-        ns2 = keep.tile([P, 1], F32, name="ns2")
-        w2b = keep.tile([P, H, FB], F32, name="w2b")
-        acc_f = keep.tile([P, B, J, H], F32, name="acc_f")
-        tau = keep.tile([P, B, J], F32, name="tau")
-        taus = keep.tile([P, B, J], F32, name="taus")
-        sig = keep.tile([P, H, B, J], F32, name="sig")
         ones = keep.tile([P, ONES], F32, name="ones")
-        sigs = keep.tile([P, H, J], F32, name="sigs")
+        warm = keep.tile([P, 1], F32, name="warm")
+        w_sq_col = keep.tile([P, H, J], F32, name="w_sq_col")
+        half_w_sq = keep.tile([P, H, K], F32, name="half_w_sq")
+        x_sq_raw = keep.tile([P, B, J], F32, name="x_sq_raw")
+        x_sq_eps = keep.tile([P, B, J], F32, name="x_sq_eps")
+        alpha_raw = keep.tile([P, 1], BF16, name="alpha_raw")
+        scale = keep.tile([P, 1], F32, name="scale")
+        scale2 = keep.tile([P, 1], F32, name="scale2")
+        neg_scale2 = keep.tile([P, 1], F32, name="neg_scale2")
+        n_over_block = keep.tile([P, B, J, H], F32, name="n_over_block")
+        n_over_features = keep.tile([P, B, J], F32, name="n_over_features")
+        x_factor = keep.tile([P, B, J], F32, name="x_factor")
+        w_factor = keep.tile([P, H, J], F32, name="w_factor")
         x_raw = keep.tile([P, B, J, D], BF16, name="x_raw")
         w_codes = keep.tile([P, H, D], U32, name="w_codes", align_bytes=64)
         w_scales = keep.tile([P, H, D], U8, name="w_scales", align_bytes=64)
         x_codes = keep.tile([P, B, D], U32, name="x_codes", align_bytes=64)
         x_scales = keep.tile([P, B, D], U8, name="x_scales", align_bytes=64)
-        f_codes = keep.tile([P, H, B * J * P], U32, name="f_codes", align_bytes=64)
-        f_scales = keep.tile([P, H, B * J * P], U8, name="f_scales", align_bytes=64)
+        f_codes = keep.tile([P, H, B, J, P], U32, name="f_codes", align_bytes=64)
+        f_scales = keep.tile([P, H, B, J, P], U8, name="f_scales", align_bytes=64)
 
-        def where(i):
-            h, g = UNITS[i // 2]
-            return h, g, i % 2
+        y_t, grad_t, z_t, q_t, r_t, m_t, n_t, dy_t, sum_t = {}, {}, {}, {}, {}, {}, {}, {}, {}
+        turned_t, back_t, dyt_t, t_codes_t, w_raw_t, piece_t = {}, {}, {}, {}, {}, {}
 
-        yt, gt, zt, qt, rt, mt, nt, dyf, dyt, bk, tcod, wraw, stg = {}, {}, {}, {}, {}, {}, {}, {}, {}, {}, {}, {}, {}
-        sums = {}
-        pfs = {}
+        def place(i):
+            b, h = UNITS[i // 2]
+            return b, h, 2 * (i % 2)
 
         def load_y(i):
-            h, g, jp = where(i)
-            y_tile = io.tile([P, 2, FB], F32, name="y_tile", bufs=6)
-            yt[i] = y_tile
-            nc.sync.dma_start(out=y_tile[:], in_=y_v[:, g, 2 * jp:2 * jp + 2, h * FB:(h + 1) * FB])
+            b, h, j = place(i)
+            y_tile = io.tile([P, 2, K], F32, name="y_tile", bufs=5)
+            y_t[i] = y_tile
+            nc.sync.dma_start(out=y_tile[:], in_=y_v[:, b, j : j + 2, h * K : (h + 1) * K])
 
-        def load_g(i):
-            h, g, jp = where(i)
-            g_tile = io.tile([P, 2, FB], BF16, name="g_tile", bufs=6)
-            gt[i] = g_tile
-            nc.sync.dma_start(out=g_tile[:], in_=g_v[:, g, 2 * jp:2 * jp + 2, h * FB:(h + 1) * FB])
+        def load_grad(i):
+            b, h, j = place(i)
+            grad_tile = io.tile([P, 2, K], BF16, name="grad_tile", bufs=5)
+            grad_t[i] = grad_tile
+            nc.sync.dma_start(out=grad_tile[:], in_=grad_v[:, b, j : j + 2, h * K : (h + 1) * K])
 
-        def load_w(h):
-            w_tile = io.tile([P, J, D], BF16, name="w_tile", bufs=3)
-            wraw[h] = w_tile
-            nc.sync.dma_start(out=w_tile[:], in_=w_v[:, h])
+        def load_weight(h):
+            w_raw = io.tile([P, J, D], BF16, name="w_raw", bufs=3)
+            w_raw_t[h] = w_raw
+            nc.sync.dma_start(out=w_raw[:], in_=weight_v[:, h])
 
-        def load_x(g):
-            nc.sync.dma_start(out=x_raw[:, g], in_=x_v[:, g])
+        def load_x(b):
+            nc.sync.dma_start(out=x_raw[:, b], in_=x_v[:, b])
 
-        def op_z(i):
-            h, g, jp = where(i)
-            z_tile = work.tile([P, 2, FB], F32, name="z_tile", bufs=2)
-            zt[i] = z_tile
-            eng = nc.gpsimd if i in () else nc.vector
-            eng.tensor_tensor(out=z_tile[:], in0=yt[i][:], in1=w2b[:, h:h + 1, :].to_broadcast([P, 2, FB]), op=ALU.subtract)
+        def spread_w_sq(h):
+            rows = psum.tile([P, J, P], F32, name="turned", bufs=2)
+            for t in range(J):
+                nc.tensor.transpose(rows[:, t, :], w_sq_col[:, h, t : t + 1].to_broadcast([P, P]), ident[:])
+            nc.vector.tensor_scalar(
+                out=half_w_sq[:, h, :].rearrange("p (m t) -> p m t", t=J), in0=rows[:].rearrange("p t m -> p m t"),
+                scalar1=0.5, scalar2=None, op0=ALU.mult)
 
-        def op_q(i):
-            h, g, jp = where(i)
-            q_tile = work.tile([P, 2, FB], F32, name="q_tile", bufs=3)
-            qt[i] = q_tile
+        def make_z(i):
+            b, h, j = place(i)
+            z_tile = work.tile([P, 2, K], F32, name="z_tile", bufs=2)
+            z_t[i] = z_tile
+            nc.vector.tensor_tensor(
+                out=z_tile[:], in0=y_t[i][:], in1=half_w_sq[:, h : h + 1, :].to_broadcast([P, 2, K]), op=ALU.subtract)
+
+        def make_q(i):
+            b, h, j = place(i)
+            q_tile = work.tile([P, 2, K], F32, name="q_tile", bufs=3)
+            q_t[i] = q_tile
             for s in range(2):
                 nc.scalar.activation(
-                    out=q_tile[:, s, :], in_=zt[i][:, s, :],
-                    func=ACT.Abs_reciprocal_sqrt, bias=xse[:, g, 2 * jp + s:2 * jp + s + 1], scale=-2.0)
+                    out=q_tile[:, s, :], in_=z_t[i][:, s, :], func=ACT.Abs_reciprocal_sqrt,
+                    bias=x_sq_eps[:, b, j + s : j + s + 1], scale=-2.0)
 
-        def op_sq(i):
-            nc.scalar.activation(out=qt[i][:], in_=qt[i][:], func=ACT.Square)
+        def square_q(i):
+            nc.scalar.activation(out=q_t[i][:], in_=q_t[i][:], func=ACT.Square)
 
-        def op_r(i):
+        def make_r(i):
             r_tile = work.tile([P, J, 2, P], F32, name="r_tile", bufs=2)
-            rt[i] = r_tile
+            r_t[i] = r_tile
             nc.vector.tensor_tensor(
                 out=r_tile[:].rearrange("p t s m -> p (s m) t"),
-                in0=yt[i][:].rearrange("p s (m t) -> p (s m) t", t=J),
-                in1=qt[i][:].rearrange("p s (m t) -> p (s m) t", t=J), op=ALU.mult)
+                in0=y_t[i][:].rearrange("p s (m t) -> p (s m) t", t=J),
+                in1=q_t[i][:].rearrange("p s (m t) -> p (s m) t", t=J), op=ALU.mult)
 
-        def op_m(i):
+        def make_m(i):
             m_tile = work.tile([P, J, 2, P], F32, name="m_tile", bufs=2)
-            mt[i] = m_tile
+            m_t[i] = m_tile
             nc.vector.tensor_tensor(
-                out=m_tile[:].rearrange("p t s (a b) -> p (s a) t b", b=4),
-                in0=rt[i][:].rearrange("p t s (a b) -> p (s a) t b", b=4),
-                in1=gt[i][:].rearrange("p s (a b t) -> p (s a) t b", b=4, t=J), op=ALU.mult)
+                out=m_tile[:].rearrange("p t s (a c) -> p (s a) t c", c=4),
+                in0=r_t[i][:].rearrange("p t s (a c) -> p (s a) t c", c=4),
+                in1=grad_t[i][:].rearrange("p s (a c t) -> p (s a) t c", c=4, t=J), op=ALU.mult)
 
-        def op_n(i, s):
-            h, g, jp = where(i)
+        def make_n(i, s):
+            b, h, j = place(i)
             if s == 0:
                 n_tile = work.tile([P, J, 2, P], F32, name="n_tile", bufs=4)
-                nt[i] = n_tile
+                n_t[i] = n_tile
             nc.vector.scalar_tensor_tensor(
-                out=nt[i][:, :, s, :], in0=mt[i][:, :, s, :], scalar=1.0, in1=rt[i][:, :, s, :],
-                op0=ALU.mult, op1=ALU.mult, accum_out=acc_f[:, g, 2 * jp + s, h:h + 1])
+                out=n_t[i][:, :, s, :], in0=m_t[i][:, :, s, :], scalar=1.0, in1=r_t[i][:, :, s, :],
+                op0=ALU.mult, op1=ALU.mult, accum_out=n_over_block[:, b, j + s, h : h + 1])
 
-        def op_fwd(i, s):
-            if s == 0:
-                f_tile = work.tile([P, 2, P, J], BF16, name="f_tile", bufs=3, align_bytes=64)
-                dyf[i] = f_tile
-            pf = psum.tile([P, J, P], F32, name="pf", bufs=2)
+        def turn(i, s):
+            turned = psum.tile([P, J, P], F32, name="turned", bufs=2)
+            turned_t[(i, s)] = turned
             for t in range(J):
-                nc.tensor.matmul(out=pf[:, t, :], lhsT=mt[i][:, t, s, :], rhs=ident[:], is_transpose=True, start=True, stop=False)
-                nc.tensor.matmul(out=pf[:, t, :], lhsT=nt[i][:, t, s, :], rhs=ident[:], is_transpose=True, start=False, stop=True)
-            pfs[(i, s)] = pf
+                nc.tensor.matmul(
+                    out=turned[:, t, :], lhsT=m_t[i][:, t, s, :], rhs=ident[:], is_transpose=True, start=True, stop=False)
+                nc.tensor.matmul(
+                    out=turned[:, t, :], lhsT=n_t[i][:, t, s, :], rhs=ident[:], is_transpose=True, start=False, stop=True)
 
-        def op_fwd_copy(i, s):
-            nc.scalar.activation(out=dyf[i][:, s], in_=pfs[(i, s)][:].rearrange("p t k -> p k t"), func=ACT.Copy, scale=s2[:, 0:1])
+        def round_dy(i, s):
+            if s == 0:
+                dy_tile = work.tile([P, 2, P, J], BF16, name="dy_tile", bufs=3, align_bytes=64)
+                dy_t[i] = dy_tile
+            nc.scalar.activation(
+                out=dy_t[i][:, s], in_=turned_t[(i, s)][:].rearrange("m t p -> m p t"), func=ACT.Copy, scale=scale2[:, 0:1])
 
-        def op_qf(i):
-            h, g, jp = where(i)
-            c0 = (g * J + 2 * jp) * P
+        def quantize_features(i):
+            b, h, j = place(i)
             nc.vector.quantize_mx(
-                out=f_codes[:, h, c0:c0 + 2 * P].bitcast(E5M2), scales=f_scales[:, h, c0:c0 + 2 * P],
-                in_=dyf[i][:].rearrange("p s k t -> p (s k t)"))
+                out=f_codes[:, h, b, j : j + 2, :].rearrange("m s p -> m (s p)").bitcast(E5M2),
+                scales=f_scales[:, h, b, j : j + 2, :].rearrange("m s p -> m (s p)"),
+                in_=dy_t[i][:].rearrange("m s p t -> m (s p t)"))
 
-        def op_back(i):
-            h, g, jp = where(i)
-            if jp == 0:
-                b0 = psum.tile([P, J * P], F32, name="b0", bufs=1)
-                b1 = psum.tile([P, J * P], F32, name="b1", bufs=1)
-                bk[i // 2] = (b0, b1)
+        def turn_back(i):
+            b, h, j = place(i)
+            if j == 0:
+                back_0 = psum.tile([P, J * P], F32, name="back_0", bufs=1)
+                back_1 = psum.tile([P, J * P], F32, name="back_1", bufs=1)
+                back_t[i // 2] = (back_0, back_1)
             for s in range(2):
-                words = dyf[i][:, s].rearrange("p k t -> p (k t)").bitcast(F32)
+                words = dy_t[i][:, s].rearrange("m p t -> m (p t)").bitcast(F32)
                 for e in range(2):
-                    j = 2 * jp + s
-                    nc.tensor.transpose(bk[i // 2][e][:, j * P:(j + 1) * P], words[:, e:2 * P:2], ident[:])
+                    nc.tensor.transpose(back_t[i // 2][e][:, (j + s) * P : (j + s + 1) * P], words[:, e : 2 * P : 2], ident[:])
 
-        def op_back_copy(u, e):
-            if e == 0:
-                t_tile = work.tile([P, J, P, J], BF16, name="t_tile", bufs=2, align_bytes=64)
-                dyt[u] = t_tile
-            nc.scalar.copy(out=dyt[u][:, 2 * e:2 * e + 2],
-                           in_=bk[u][e][:].bitcast(BF16).rearrange("p (j m i) -> p i m j", j=J, i=2))
+        def gather_slots(u):
+            dyt_tile = work.tile([P, J, P, J], BF16, name="dyt_tile", bufs=2, align_bytes=64)
+            dyt_t[u] = dyt_tile
+            for e in range(2):
+                nc.scalar.copy(
+                    out=dyt_tile[:, 2 * e : 2 * e + 2],
+                    in_=back_t[u][e][:].bitcast(BF16).rearrange("p (j m i) -> p i m j", j=J, i=2))
 
-        def op_qt(u):
-            t_codes = work.tile([P, FB], U32, name="t_codes", bufs=4, align_bytes=64)
-            t_scales = work.tile([P, FB], U8, name="t_scales", bufs=4, align_bytes=64)
-            tcod[UNITS[u]] = (t_codes, t_scales)
-            nc.vector.quantize_mx(out=t_codes[:].bitcast(E5M2), scales=t_scales[:], in_=dyt[u][:].rearrange("p t m j -> p (t m j)"))
+        def quantize_tokens(u):
+            t_codes = work.tile([P, K], U32, name="t_codes", bufs=6, align_bytes=64)
+            t_scales = work.tile([P, K], U8, name="t_scales", bufs=6, align_bytes=64)
+            t_codes_t[UNITS[u]] = (t_codes, t_scales)
+            nc.vector.quantize_mx(
+                out=t_codes[:].bitcast(E5M2), scales=t_scales[:], in_=dyt_t[u][:].rearrange("p t m j -> p (t m j)"))
 
-        def op_sum(u, t):
+        def sum_tokens(u, t):
             if t == 0:
-                ps = psum.tile([P, J, ONES], F32, name="ps", bufs=1)
-                sums[u] = ps
-            for k in range(4):
-                i, s = 2 * u + k // 2, k % 2
-                nc.tensor.matmul(out=sums[u][:, t, :], lhsT=nt[i][:, t, s, :], rhs=ones[:], start=(k == 0), stop=(k == 3))
+                sums = psum.tile([P, J, ONES], F32, name="sums", bufs=1)
+                sum_t[u] = sums
+            for k in range(J):
+                nc.tensor.matmul(
+                    out=sum_t[u][:, t, :], lhsT=n_t[2 * u + k // 2][:, t, k % 2, :], rhs=ones[:],
+                    start=(k == 0), stop=(k == J - 1))
 
-        def op_sum_scale(u):
-            h, g = UNITS[u]
-            nc.vector.tensor_scalar(out=sig[:, h, g, :], in0=sums[u][:, :, 0:1].rearrange("p t o -> p (t o)"), scalar1=ns2[:, 0:1], scalar2=None, op0=ALU.mult)
-
-        def op_sig(h):
-            nc.vector.tensor_tensor(out=sigs[:, h, :], in0=sig[:, h, 0, :], in1=sig[:, h, 1, :], op=ALU.add)
-
-        def op_tau(i):
-            h, g, jp = where(i)
-            nc.vector.tensor_reduce(out=tau[:, g, 2 * jp:2 * jp + 2], in_=acc_f[:, g, 2 * jp:2 * jp + 2, :], axis=AX.X, op=ALU.add)
-            nc.vector.tensor_scalar(out=taus[:, g, 2 * jp:2 * jp + 2], in0=tau[:, g, 2 * jp:2 * jp + 2], scalar1=ns2[:, 0:1], scalar2=None, op0=ALU.mult)
-
-        SW = 256
-        pieces = [("x", g, n) for g in range(B) for n in range(D // SW)] + [("w", h, n) for h in range(H) for n in range(D // SW)]
-
-        def op_stage(k, eng):
-            kind, a, n = pieces[k]
-            s_tile = work.tile([P, SW, J], BF16, name="s_tile", bufs=4, align_bytes=64)
-            stg[k] = s_tile
-            src = x_raw[:, a, :, n * SW:(n + 1) * SW] if kind == "x" else wraw[a][:, :, n * SW:(n + 1) * SW]
-            if eng == "v":
-                nc.vector.tensor_copy(out=s_tile[:].rearrange("p (c i) j -> p c j i", i=4), in_=src.rearrange("p j (c i) -> p c j i", i=4))
+        def add_token_sums(u):
+            b, h = UNITS[u]
+            sums = sum_t[u][:, :, 0:1].rearrange("m t o -> m (t o)")
+            if b == 0:
+                nc.vector.tensor_scalar(
+                    out=w_factor[:, h, :], in0=sums, scalar1=neg_scale2[:, 0:1], scalar2=None, op0=ALU.mult)
             else:
-                nc.scalar.copy(out=s_tile[:].rearrange("p (c i) j -> p c j i", i=4), in_=src.rearrange("p j (c i) -> p c j i", i=4))
+                nc.vector.scalar_tensor_tensor(
+                    out=w_factor[:, h, :], in0=sums, scalar=neg_scale2[:, 0:1], in1=w_factor[:, h, :], op0=ALU.mult, op1=ALU.add)
 
-        def op_stage_q(k):
-            kind, a, n = pieces[k]
-            codes, scales = (x_codes, x_scales) if kind == "x" else (w_codes, w_scales)
-            nc.vector.quantize_mx(out=codes[:, a, n * SW:(n + 1) * SW].bitcast(E4M3), scales=scales[:, a, n * SW:(n + 1) * SW],
-                                  in_=stg[k][:].rearrange("p d j -> p (d j)"))
+        pieces = [("weight", h, c) for h in range(H) for c in range(0, D, PIECE)]
+        pieces += [("x", b, c) for b in range(B) for c in range(0, D, PIECE)]
 
-        ready = []
-        pending = []
-        outs = {}
-        tail = []
-        nbufs = {"acc": MX_BANKS, "pf": 2, "b0": 1, "b1": 1, "ps": 1}
-
-        def emit_mm():
-            kind, a, b, n = ready.pop(0)
-            tag = "acc"
-            if tail:
-                tag = tail.pop(0)
-                tail.append(tag)
-            acc = psum.tile([P, NT], F32, name=tag, bufs=nbufs[tag])
-            cols = slice(n * NT, (n + 1) * NT)
-            if kind == 1:
-                for g in range(B):
-                    codes, scales = tcod[(a, g)]
-                    nc.tensor.matmul_mx(out=acc[:], lhsT=codes[:, b * P:(b + 1) * P].bitcast(E5M2), lhsT_scale=scales[:, b * P:(b + 1) * P],
-                                        rhs=x_codes[:, g, cols].bitcast(E4M3), rhs_scale=x_scales[:, g, cols], start=(g == 0), stop=(g == B - 1))
+        def copy_piece(k, on_vector):
+            kind, a, c = pieces[k]
+            piece = work.tile([P, PIECE, J], BF16, name="piece", bufs=4, align_bytes=64)
+            piece_t[k] = piece
+            rows = w_raw_t[a][:, :, c : c + PIECE] if kind == "weight" else x_raw[:, a, :, c : c + PIECE]
+            out = piece[:].rearrange("p (c i) j -> p c j i", i=4)
+            in_ = rows.rearrange("p j (c i) -> p c j i", i=4)
+            if on_vector:
+                nc.vector.tensor_copy(out=out, in_=in_)
             else:
-                toks = slice((a * J + b) * P, (a * J + b + 1) * P)
+                nc.scalar.copy(out=out, in_=in_)
+
+        def quantize_piece(k):
+            kind, a, c = pieces[k]
+            codes, scales = (w_codes, w_scales) if kind == "weight" else (x_codes, x_scales)
+            nc.vector.quantize_mx(
+                out=codes[:, a, c : c + PIECE].bitcast(E4M3), scales=scales[:, a, c : c + PIECE],
+                in_=piece_t[k][:].rearrange("p d j -> p (d j)"))
+
+        ready, issued = [], []
+        calls = [0]
+
+        def issue_product():
+            kind, a, c, col = ready.pop(0)
+            acc = psum.tile([P, N], F32, name="acc", bufs=ACC_BANKS)
+            cols = slice(col, col + N)
+            if kind == "out_1":
+                for b in range(B):
+                    codes, scales = t_codes_t[(b, a)]
+                    nc.tensor.matmul_mx(
+                        out=acc[:],
+                        lhsT=codes[:, c * P : (c + 1) * P].bitcast(E5M2), lhsT_scale=scales[:, c * P : (c + 1) * P],
+                        rhs=x_codes[:, b, cols].bitcast(E4M3), rhs_scale=x_scales[:, b, cols],
+                        start=(b == 0), stop=(b == B - 1))
+            else:
                 for h in range(H):
-                    nc.tensor.matmul_mx(out=acc[:], lhsT=f_codes[:, h, toks].bitcast(E5M2), lhsT_scale=f_scales[:, h, toks],
-                                        rhs=w_codes[:, h, cols].bitcast(E4M3), rhs_scale=w_scales[:, h, cols], start=(h == 0), stop=(h == H - 1))
-            pending.append((kind, a, b, n, acc))
+                    nc.tensor.matmul_mx(
+                        out=acc[:],
+                        lhsT=f_codes[:, h, a, c, :].bitcast(E5M2), lhsT_scale=f_scales[:, h, a, c, :],
+                        rhs=w_codes[:, h, cols].bitcast(E4M3), rhs_scale=w_scales[:, h, cols],
+                        start=(h == 0), stop=(h == H - 1))
+            issued.append((calls[0], kind, a, c, col, acc))
 
-        def emit_stt():
-            kind, a, b, n, acc = pending.pop(0)
-            cols = slice(n * NT, (n + 1) * NT)
-            if n == 0:
-                o_tile = io.tile([P, D], F32, name="o_tile", bufs=4)
-                outs[(kind, a, b)] = o_tile
-            o = outs[(kind, a, b)]
-            if kind == 1:
-                raw, fac, dst = wraw[a][:, b, cols], sigs[:, a, b:b + 1], o1_v[:, a, b]
+        def finish_product():
+            kind, a, c, col, acc = issued.pop(0)[1:]
+            cols = slice(col, col + N)
+            if kind == "out_1":
+                rows, factor, out = w_raw_t[a][:, c, cols], w_factor[:, a, c : c + 1], out_1_v[:, a, c, cols]
             else:
-                raw, fac, dst = x_raw[:, a, b, cols], taus[:, a, b:b + 1], o0_v[:, a, b]
-            nc.vector.scalar_tensor_tensor(out=o[:, cols], in0=raw, scalar=fac, in1=acc[:], op0=ALU.mult, op1=ALU.add)
-            if n == 1:
-                nc.sync.dma_start(out=dst, in_=o[:])
+                rows, factor, out = x_raw[:, a, c, cols], x_factor[:, a, c : c + 1], out_0_v[:, a, c, cols]
+            result = io.tile([P, N], F32, name="result", bufs=8)
+            nc.vector.scalar_tensor_tensor(out=result[:], in0=rows, scalar=factor, in1=acc[:], op0=ALU.mult, op1=ALU.add)
+            nc.sync.dma_start(out=out, in_=result[:])
 
-        def some_stt():
-            if pending:
-                emit_stt()
+        def next_product(lag=READ_LAG):
+            calls[0] += 1
+            if issued and calls[0] - issued[0][0] >= lag:
+                finish_product()
+            if ready and len(issued) < ACC_BANKS:
+                issue_product()
+
+        def feature_side(i):
+            b, h, j = place(i)
+            last = h == H - 1
+            slots = slice(j, j + 2)
+            if last:
+                nc.vector.tensor_reduce(
+                    out=n_over_features[:, b, slots], in_=n_over_block[:, b, slots, :], axis=AX.X, op=ALU.add)
+            quantize_features(i)
+            if last:
+                nc.vector.tensor_scalar(
+                    out=x_factor[:, b, slots], in0=n_over_features[:, b, slots], scalar1=neg_scale2[:, 0:1],
+                    scalar2=None, op0=ALU.mult)
+                ready.extend([("out_0", b, j + s, col) for s in range(2) for col in range(0, D, N)])
+
+        def token_side(u):
+            b, h = UNITS[u]
+            quantize_tokens(u)
+            add_token_sums(u)
+            if b == B - 1:
+                ready.extend([("out_1", h, t, col) for t in range(J) for col in range(0, D, N)])
 
         with tc.manual_schedule():
-            nc.sync.dma_start(out=wcol[:], in_=w_sq.rearrange("(h m t) -> m h t", h=H, t=J))
-            nc.sync.dma_start(out=xsq[:], in_=x_sq.rearrange("g (p j) o -> p g (j o)", j=J))
-            nc.sync.dma_start(out=al[:], in_=alpha.partition_broadcast(P))
+            nc.sync.dma_start(out=w_sq_col[:], in_=w_sq.rearrange("(h m t) -> m h t", h=H, t=J))
+            nc.sync.dma_start(out=x_sq_raw[:], in_=x_sq.rearrange("b (p j) o -> p b (j o)", j=J))
+            nc.sync.dma_start(out=alpha_raw[:], in_=alpha.partition_broadcast(P))
             load_y(0)
-            make_identity(nc, ident[:])
-            nc.vector.memset(junk[:], 1.0)
-            nc.vector.memset(ones[:], 1.0)
-            nc.scalar.activation(out=junk[:], in_=junk[:], func=ACT.Exp)
             load_y(1)
-            load_g(0)
-
-            def spread(h, eng):
-                pw = psum.tile([P, J, P], F32, name="pf", bufs=2)
-                for t in range(J):
-                    nc.tensor.transpose(pw[:, t, :], wcol[:, h, t:t + 1].to_broadcast([P, P]), ident[:])
-                dst, srcp = w2b[:, h, :].rearrange("p (m t) -> p m t", t=J), pw[:].rearrange("p t m -> p m t")
-                if eng == "v":
-                    nc.vector.tensor_scalar(out=dst, in0=srcp, scalar1=0.5, scalar2=None, op0=ALU.mult)
-                else:
-                    nc.scalar.activation(out=dst, in_=srcp, func=ACT.Copy, scale=0.5)
-
-            nc.scalar.activation(out=sc[:], in_=al[:], func=ACT.Exp, scale=LOG_BASE)
-            nc.scalar.activation(out=junk[:], in_=junk[:], func=ACT.Abs_reciprocal_sqrt)
-            nc.vector.tensor_scalar(out=xse[:], in0=xsq[:], scalar1=EPS, scalar2=None, op0=ALU.add)
-            spread(0, "v")
+            load_grad(0)
             load_y(2)
-            load_g(1)
+            load_grad(1)
             load_y(3)
-            load_g(2)
-            load_g(3)
-            load_x(0)
-            nloaded = 4
-            QL, ZL = 2, 3
-            for k in range(QL):
-                op_z(k)
-                if k == 0:
-                    spread(1, "v")
-                    nc.vector.tensor_scalar(out=s2[:], in0=sc[:], scalar1=2.0, scalar2=None, op0=ALU.mult)
-                    nc.vector.tensor_scalar(out=ns2[:], in0=sc[:], scalar1=-2.0, scalar2=None, op0=ALU.mult)
-            for k in range(QL):
-                op_q(k)
-                op_sq(k)
-            spread(2, "v")
-            spread(3, "v")
-            def feature_side(i):
-                op_qf(i)
-                if UNITS[i // 2] in LAST_F:
-                    op_tau(i)
-                    h, g, jp = where(i)
-                    ready.extend([(0, g, 2 * jp + s, n) for s in range(2) for n in range(2)])
+            load_grad(2)
+            load_grad(3)
+            load_weight(0)
 
-            def pump():
-                some_stt()
-                if ready and len(pending) < MX_BANKS:
-                    emit_mm()
+            make_identity(nc, ident[:])
+            nc.vector.memset(warm[:], 1.0)
+            nc.vector.memset(ones[:], 1.0)
+            nc.scalar.activation(out=warm[:], in_=warm[:], func=ACT.Exp)
+            nc.scalar.activation(out=scale[:], in_=alpha_raw[:], func=ACT.Exp, scale=LOG_BASE)
+            nc.scalar.activation(out=warm[:], in_=warm[:], func=ACT.Abs_reciprocal_sqrt)
+            nc.vector.tensor_scalar(out=x_sq_eps[:], in0=x_sq_raw[:], scalar1=EPS, scalar2=None, op0=ALU.add)
+            spread_w_sq(0)
+            make_z(0)
+            spread_w_sq(1)
+            nc.vector.tensor_scalar(out=scale2[:], in0=scale[:], scalar1=2.0, scalar2=None, op0=ALU.mult)
+            nc.vector.tensor_scalar(out=neg_scale2[:], in0=scale[:], scalar1=-2.0, scalar2=None, op0=ALU.mult)
+            make_z(1)
+            for i in range(2):
+                make_q(i)
+                square_q(i)
+            spread_w_sq(2)
+            spread_w_sq(3)
 
-            nstage = 0
-            nquant = 0
-            nw = 0
-            for i in range(PAIRS + 2):
-                live = i < PAIRS
-                while nloaded < min(PAIRS, i + 5):
-                    load_y(nloaded)
-                    load_g(nloaded)
-                    nloaded += 1
+            copied = quantized = 0
+            for i in range(STEPS):
+                if i + 4 < STEPS:
+                    load_y(i + 4)
+                    load_grad(i + 4)
+                if i < 2 * (H - 1) and i % 2 == 0:
+                    load_weight(i // 2 + 1)
+                if 0 <= i - 5 < B:
+                    load_x(i - 5)
+                if i >= STEPS // 2 and i % 2 == 0:
+                    load_weight(i // 2 - H)
+
+                if i >= 1:
+                    turn(i - 1, 0)
+                    turn(i - 1, 1)
+                make_r(i)
                 if i == 0:
-                    load_x(1)
-                while nw < H and i >= (0, 2, 4, 7)[nw]:
-                    load_w(nw)
-                    nw += 1
-                prev = 1 <= i < PAIRS + 1
-                if prev:
-                    op_fwd(i - 1, 0)
-                    op_fwd(i - 1, 1)
-                if live:
-                    op_r(i)
-                if i == 0:
-                    for k in range(QL, ZL):
-                        op_z(k)
-                if i + QL < PAIRS:
-                    op_q(i + QL)
-                if 2 <= i < PAIRS + 2:
-                    op_sum((i - 2) // 2, 2 * (i % 2))
-                    if i % 2 == 1:
-                        op_sum((i - 2) // 2, 3)
-                if prev:
-                    op_fwd_copy(i - 1, 0)
-                    op_fwd_copy(i - 1, 1)
-                    op_back(i - 1)
-                if 2 <= i < PAIRS + 2 and i % 2 == 0:
-                    op_sum((i - 2) // 2, 1)
-                if i + QL < PAIRS:
-                    op_sq(i + QL)
-                if i + ZL < PAIRS:
-                    op_z(i + ZL)
-                if live:
-                    op_m(i)
-                pump()
-                while nquant < nstage - (1, 1, 1, 1, 1, 1, 1, 1, 1, 1, 1, 1, 0, 0, 0, 0)[min(i, 15)]:
-                    op_stage_q(nquant)
-                    nquant += 1
-                if 2 <= i < PAIRS:
+                    make_z(2)
+                if i + 2 < STEPS:
+                    make_q(i + 2)
+                if i >= 2:
+                    unit = (i - 2) // 2
+                    for t in (2, 3) if i % 2 else (0,):
+                        sum_tokens(unit, t)
+                if i >= 1:
+                    round_dy(i - 1, 0)
+                    round_dy(i - 1, 1)
+                    turn_back(i - 1)
+                if i >= 2 and i % 2 == 0:
+                    sum_tokens((i - 2) // 2, 1)
+                if i + 2 < STEPS:
+                    square_q(i + 2)
+                if i + 3 < STEPS:
+                    make_z(i + 3)
+                make_m(i)
+                next_product()
+                hold = 0 if i in (WEIGHT_NEEDED, X_NEEDED) else 1
+                while quantized < copied - hold:
+                    quantize_piece(quantized)
+                    quantized += 1
+                if i >= 2:
                     feature_side(i - 2)
-                pump()
-                if 3 <= i < PAIRS + 3 and i % 2 == 1:
-                    u = (i - 3) // 2
-                    op_qt(u)
-                    op_sum_scale(u)
-                    if UNITS[u] in LAST_T:
-                        op_sig(UNITS[u][0])
-                    if UNITS[u] in LAST_T:
-                        ready.extend([(1, UNITS[u][0], t, n) for t in range(J) for n in range(2)])
-                for k in range((0, 0, 0, 0, 0, 0, 0, 0, 0, 0, 0, 0, 0, 0, 0, 0)[min(i, 15)]):
-                    op_stage(nstage, "v")
-                    nstage += 1
-                if live:
-                    op_n(i, 0)
-                pump()
-                if live:
-                    op_n(i, 1)
-                pump()
-                if i >= PAIRS - 1 and prev:
+                if i == STEPS - 1:
+                    next_product()
                     feature_side(i - 1)
-                if prev and i % 2 == 0:
-                    op_back_copy((i - 1) // 2, 0)
-                    op_back_copy((i - 1) // 2, 1)
-                for k in range((2, 2, 2, 2, 2, 2, 2, 2, 2, 2, 2, 2, 0, 0, 0, 0)[min(i, 15)]):
-                    if nstage < len(pieces):
-                        op_stage(nstage, "s")
-                        nstage += 1
-                if i >= PAIRS + 1 and not tail:
-                    tail.extend(["acc", "pf", "acc", "b0", "acc", "b1", "pf", "ps"])
-                while ready and len(pending) < (MX_BANKS if not tail else 7):
-                    emit_mm()
-                for k in range((0, 0, 0, 0, 0, 0, 0, 0, 0, 0, 0, 0, 0, 1, 2, 0, 0, 0, 0)[i] if i < len((0, 0, 0, 0, 0, 0, 0, 0, 0, 0, 0, 0, 0, 1, 2, 0, 0, 0, 0)) else 0):
-                    pump()
-                    if ready:
-                        emit_mm()
-            while ready or pending:
-                emit_stt()
-                if ready:
-                    emit_mm()
+                next_product()
+                if i >= 3 and i % 2 == 1:
+                    token_side((i - 3) // 2)
+                if i in VECTOR_STEPS:
+                    copy_piece(copied, on_vector=True)
+                    copied += 1
+                make_n(i, 0)
+                next_product()
+                make_n(i, 1)
+                next_product()
+                if i >= 2 and i % 2 == 0:
+                    gather_slots((i - 2) // 2)
+                for k in range(SCALAR_PIECES[i]):
+                    copy_piece(copied, on_vector=False)
+                    copied += 1
+                next_product()
+
+            last = STEPS - 1
+            for s in range(2):
+                turn(last, s)
+            for s in range(2):
+                round_dy(last, s)
+            for k in range(2):
+                next_product(lag=1)
+            turn_back(last)
+            gather_slots(last // 2)
+            for k in range(2):
+                next_product(lag=1)
+            feature_side(last)
+            for k in range(2):
+                next_product(lag=1)
+            for t in range(J):
+                sum_tokens(last // 2, t)
+            for k in range(2):
+                next_product(lag=1)
+            token_side(last // 2)
+            while ready or issued:
+                next_product(lag=1)

import math
from contextlib import ExitStack

import concourse.mybir as mybir
from concourse.masks import make_identity

B, S, D, F = 2, 512, 1024, 2048
FLOPS = 2 * 2 * B * S * D * F
BYTES = 2 * (B * S * D + F * D + B * S * F) + 4 * (B * S * F + B * S + F) + 2 + 4 * (B * S * D + F * D)

P = 128
J = 4
K = P * J
H = F // K
N = 512
EPS = 1e-6
LOG_BASE = math.log(math.sqrt(F) / math.log(1.0 + F))

F32 = mybir.dt.float32
BF16 = mybir.dt.bfloat16
U32 = mybir.dt.uint32
U8 = mybir.dt.uint8
E4M3 = mybir.dt.float8_e4m3fn_x4
E5M2 = mybir.dt.float8_e5m2_x4
ACT = mybir.ActivationFunctionType
ALU = mybir.AluOpType
AX = mybir.AxisListType

UNITS = tuple((b, h) for b in range(B) for h in range(H))
STEPS = 2 * len(UNITS)

PIECE = 256
SCALAR_PIECES = (1, 1, 1, 1, 1, 2, 2, 2, 2, 3, 3, 0, 0, 0, 0, 0)
VECTOR_STEPS = range(1, 6)
WEIGHT_NEEDED = 2 * H
X_NEEDED = 2 * H + 3

ACC_BANKS = 3
READ_LAG = 4
ONES = 64


def tile_yatdense_v_kernel(tc, x, weight, alpha, bias, y, x_sq, w_sq, grad_out, out_0, out_1):
    nc = tc.nc
    x_v = x.rearrange("b (p j) d -> p b j d", j=J)
    weight_v = weight.rearrange("(h m t) d -> m h t d", h=H, t=J)
    y_v = y.rearrange("b (p j) f -> p b j f", j=J)
    grad_v = grad_out.rearrange("b (p j) f -> p b j f", j=J)
    out_0_v = out_0.rearrange("b (p j) d -> p b j d", j=J)
    out_1_v = out_1.rearrange("(h m t) d -> m h t d", h=H, t=J)

    with ExitStack() as ctx:
        keep = ctx.enter_context(tc.tile_pool(name="keep", bufs=1))
        io = ctx.enter_context(tc.tile_pool(name="io", bufs=5))
        work = ctx.enter_context(tc.tile_pool(name="work", bufs=2))
        psum = ctx.enter_context(tc.psum_pool(name="psum", bufs=1))

        ident = keep.tile([P, P], F32, name="ident")
        ones = keep.tile([P, ONES], F32, name="ones")
        warm = keep.tile([P, 1], F32, name="warm")
        w_sq_col = keep.tile([P, H, J], F32, name="w_sq_col")
        half_w_sq = keep.tile([P, H, K], F32, name="half_w_sq")
        x_sq_raw = keep.tile([P, B, J], F32, name="x_sq_raw")
        x_sq_eps = keep.tile([P, B, J], F32, name="x_sq_eps")
        alpha_raw = keep.tile([P, 1], BF16, name="alpha_raw")
        scale = keep.tile([P, 1], F32, name="scale")
        scale2 = keep.tile([P, 1], F32, name="scale2")
        neg_scale2 = keep.tile([P, 1], F32, name="neg_scale2")
        n_over_block = keep.tile([P, B, J, H], F32, name="n_over_block")
        n_over_features = keep.tile([P, B, J], F32, name="n_over_features")
        x_factor = keep.tile([P, B, J], F32, name="x_factor")
        w_factor = keep.tile([P, H, J], F32, name="w_factor")
        x_raw = keep.tile([P, B, J, D], BF16, name="x_raw")
        w_codes = keep.tile([P, H, D], U32, name="w_codes", align_bytes=64)
        w_scales = keep.tile([P, H, D], U8, name="w_scales", align_bytes=64)
        x_codes = keep.tile([P, B, D], U32, name="x_codes", align_bytes=64)
        x_scales = keep.tile([P, B, D], U8, name="x_scales", align_bytes=64)
        f_codes = keep.tile([P, H, B, J, P], U32, name="f_codes", align_bytes=64)
        f_scales = keep.tile([P, H, B, J, P], U8, name="f_scales", align_bytes=64)

        y_t, grad_t, z_t, q_t, r_t, m_t, n_t, dy_t, sum_t = {}, {}, {}, {}, {}, {}, {}, {}, {}
        turned_t, back_t, dyt_t, t_codes_t, w_raw_t, piece_t = {}, {}, {}, {}, {}, {}

        def place(i):
            b, h = UNITS[i // 2]
            return b, h, 2 * (i % 2)

        def load_y(i):
            b, h, j = place(i)
            y_tile = io.tile([P, 2, K], F32, name="y_tile", bufs=5)
            y_t[i] = y_tile
            nc.sync.dma_start(out=y_tile[:], in_=y_v[:, b, j : j + 2, h * K : (h + 1) * K])

        def load_grad(i):
            b, h, j = place(i)
            grad_tile = io.tile([P, 2, K], BF16, name="grad_tile", bufs=5)
            grad_t[i] = grad_tile
            nc.sync.dma_start(out=grad_tile[:], in_=grad_v[:, b, j : j + 2, h * K : (h + 1) * K])

        def load_weight(h):
            w_raw = io.tile([P, J, D], BF16, name="w_raw", bufs=3)
            w_raw_t[h] = w_raw
            nc.sync.dma_start(out=w_raw[:], in_=weight_v[:, h])

        def load_x(b):
            nc.sync.dma_start(out=x_raw[:, b], in_=x_v[:, b])

        def spread_w_sq(h):
            rows = psum.tile([P, J, P], F32, name="turned", bufs=2)
            for t in range(J):
                nc.tensor.transpose(rows[:, t, :], w_sq_col[:, h, t : t + 1].to_broadcast([P, P]), ident[:])
            nc.vector.tensor_scalar(
                out=half_w_sq[:, h, :].rearrange("p (m t) -> p m t", t=J), in0=rows[:].rearrange("p t m -> p m t"),
                scalar1=0.5, scalar2=None, op0=ALU.mult)

        def make_z(i):
            b, h, j = place(i)
            z_tile = work.tile([P, 2, K], F32, name="z_tile", bufs=2)
            z_t[i] = z_tile
            nc.vector.tensor_tensor(
                out=z_tile[:], in0=y_t[i][:], in1=half_w_sq[:, h : h + 1, :].to_broadcast([P, 2, K]), op=ALU.subtract)

        def make_q(i):
            b, h, j = place(i)
            q_tile = work.tile([P, 2, K], F32, name="q_tile", bufs=3)
            q_t[i] = q_tile
            for s in range(2):
                nc.scalar.activation(
                    out=q_tile[:, s, :], in_=z_t[i][:, s, :], func=ACT.Abs_reciprocal_sqrt,
                    bias=x_sq_eps[:, b, j + s : j + s + 1], scale=-2.0)

        def square_q(i):
            nc.scalar.activation(out=q_t[i][:], in_=q_t[i][:], func=ACT.Square)

        def make_r(i):
            r_tile = work.tile([P, J, 2, P], F32, name="r_tile", bufs=2)
            r_t[i] = r_tile
            nc.vector.tensor_tensor(
                out=r_tile[:].rearrange("p t s m -> p (s m) t"),
                in0=y_t[i][:].rearrange("p s (m t) -> p (s m) t", t=J),
                in1=q_t[i][:].rearrange("p s (m t) -> p (s m) t", t=J), op=ALU.mult)

        def make_m(i):
            m_tile = work.tile([P, J, 2, P], F32, name="m_tile", bufs=2)
            m_t[i] = m_tile
            nc.vector.tensor_tensor(
                out=m_tile[:].rearrange("p t s (a c) -> p (s a) t c", c=4),
                in0=r_t[i][:].rearrange("p t s (a c) -> p (s a) t c", c=4),
                in1=grad_t[i][:].rearrange("p s (a c t) -> p (s a) t c", c=4, t=J), op=ALU.mult)

        def make_n(i, s):
            b, h, j = place(i)
            if s == 0:
                n_tile = work.tile([P, J, 2, P], F32, name="n_tile", bufs=4)
                n_t[i] = n_tile
            nc.vector.scalar_tensor_tensor(
                out=n_t[i][:, :, s, :], in0=m_t[i][:, :, s, :], scalar=1.0, in1=r_t[i][:, :, s, :],
                op0=ALU.mult, op1=ALU.mult, accum_out=n_over_block[:, b, j + s, h : h + 1])

        def turn(i, s):
            turned = psum.tile([P, J, P], F32, name="turned", bufs=2)
            turned_t[(i, s)] = turned
            for t in range(J):
                nc.tensor.matmul(
                    out=turned[:, t, :], lhsT=m_t[i][:, t, s, :], rhs=ident[:], is_transpose=True, start=True, stop=False)
                nc.tensor.matmul(
                    out=turned[:, t, :], lhsT=n_t[i][:, t, s, :], rhs=ident[:], is_transpose=True, start=False, stop=True)

        def round_dy(i, s):
            if s == 0:
                dy_tile = work.tile([P, 2, P, J], BF16, name="dy_tile", bufs=3, align_bytes=64)
                dy_t[i] = dy_tile
            nc.scalar.activation(
                out=dy_t[i][:, s], in_=turned_t[(i, s)][:].rearrange("m t p -> m p t"), func=ACT.Copy, scale=scale2[:, 0:1])

        def quantize_features(i):
            b, h, j = place(i)
            nc.vector.quantize_mx(
                out=f_codes[:, h, b, j : j + 2, :].rearrange("m s p -> m (s p)").bitcast(E5M2),
                scales=f_scales[:, h, b, j : j + 2, :].rearrange("m s p -> m (s p)"),
                in_=dy_t[i][:].rearrange("m s p t -> m (s p t)"))

        def turn_back(i):
            b, h, j = place(i)
            if j == 0:
                back_0 = psum.tile([P, J * P], F32, name="back_0", bufs=1)
                back_1 = psum.tile([P, J * P], F32, name="back_1", bufs=1)
                back_t[i // 2] = (back_0, back_1)
            for s in range(2):
                words = dy_t[i][:, s].rearrange("m p t -> m (p t)").bitcast(F32)
                for e in range(2):
                    nc.tensor.transpose(back_t[i // 2][e][:, (j + s) * P : (j + s + 1) * P], words[:, e : 2 * P : 2], ident[:])

        def gather_slots(u):
            dyt_tile = work.tile([P, J, P, J], BF16, name="dyt_tile", bufs=2, align_bytes=64)
            dyt_t[u] = dyt_tile
            for e in range(2):
                nc.scalar.copy(
                    out=dyt_tile[:, 2 * e : 2 * e + 2],
                    in_=back_t[u][e][:].bitcast(BF16).rearrange("p (j m i) -> p i m j", j=J, i=2))

        def quantize_tokens(u):
            t_codes = work.tile([P, K], U32, name="t_codes", bufs=6, align_bytes=64)
            t_scales = work.tile([P, K], U8, name="t_scales", bufs=6, align_bytes=64)
            t_codes_t[UNITS[u]] = (t_codes, t_scales)
            nc.vector.quantize_mx(
                out=t_codes[:].bitcast(E5M2), scales=t_scales[:], in_=dyt_t[u][:].rearrange("p t m j -> p (t m j)"))

        def sum_tokens(u, t):
            if t == 0:
                sums = psum.tile([P, J, ONES], F32, name="sums", bufs=1)
                sum_t[u] = sums
            for k in range(J):
                nc.tensor.matmul(
                    out=sum_t[u][:, t, :], lhsT=n_t[2 * u + k // 2][:, t, k % 2, :], rhs=ones[:],
                    start=(k == 0), stop=(k == J - 1))

        def add_token_sums(u):
            b, h = UNITS[u]
            sums = sum_t[u][:, :, 0:1].rearrange("m t o -> m (t o)")
            if b == 0:
                nc.vector.tensor_scalar(
                    out=w_factor[:, h, :], in0=sums, scalar1=neg_scale2[:, 0:1], scalar2=None, op0=ALU.mult)
            else:
                nc.vector.scalar_tensor_tensor(
                    out=w_factor[:, h, :], in0=sums, scalar=neg_scale2[:, 0:1], in1=w_factor[:, h, :], op0=ALU.mult, op1=ALU.add)

        pieces = [("weight", h, c) for h in range(H) for c in range(0, D, PIECE)]
        pieces += [("x", b, c) for b in range(B) for c in range(0, D, PIECE)]

        def copy_piece(k, on_vector):
            kind, a, c = pieces[k]
            piece = work.tile([P, PIECE, J], BF16, name="piece", bufs=4, align_bytes=64)
            piece_t[k] = piece
            rows = w_raw_t[a][:, :, c : c + PIECE] if kind == "weight" else x_raw[:, a, :, c : c + PIECE]
            out = piece[:].rearrange("p (c i) j -> p c j i", i=4)
            in_ = rows.rearrange("p j (c i) -> p c j i", i=4)
            if on_vector:
                nc.vector.tensor_copy(out=out, in_=in_)
            else:
                nc.scalar.copy(out=out, in_=in_)

        def quantize_piece(k):
            kind, a, c = pieces[k]
            codes, scales = (w_codes, w_scales) if kind == "weight" else (x_codes, x_scales)
            nc.vector.quantize_mx(
                out=codes[:, a, c : c + PIECE].bitcast(E4M3), scales=scales[:, a, c : c + PIECE],
                in_=piece_t[k][:].rearrange("p d j -> p (d j)"))

        ready, issued = [], []
        calls = [0]

        def issue_product():
            kind, a, c, col = ready.pop(0)
            acc = psum.tile([P, N], F32, name="acc", bufs=ACC_BANKS)
            cols = slice(col, col + N)
            if kind == "out_1":
                for b in range(B):
                    codes, scales = t_codes_t[(b, a)]
                    nc.tensor.matmul_mx(
                        out=acc[:],
                        lhsT=codes[:, c * P : (c + 1) * P].bitcast(E5M2), lhsT_scale=scales[:, c * P : (c + 1) * P],
                        rhs=x_codes[:, b, cols].bitcast(E4M3), rhs_scale=x_scales[:, b, cols],
                        start=(b == 0), stop=(b == B - 1))
            else:
                for h in range(H):
                    nc.tensor.matmul_mx(
                        out=acc[:],
                        lhsT=f_codes[:, h, a, c, :].bitcast(E5M2), lhsT_scale=f_scales[:, h, a, c, :],
                        rhs=w_codes[:, h, cols].bitcast(E4M3), rhs_scale=w_scales[:, h, cols],
                        start=(h == 0), stop=(h == H - 1))
            issued.append((calls[0], kind, a, c, col, acc))

        def finish_product():
            kind, a, c, col, acc = issued.pop(0)[1:]
            cols = slice(col, col + N)
            if kind == "out_1":
                rows, factor, out = w_raw_t[a][:, c, cols], w_factor[:, a, c : c + 1], out_1_v[:, a, c, cols]
            else:
                rows, factor, out = x_raw[:, a, c, cols], x_factor[:, a, c : c + 1], out_0_v[:, a, c, cols]
            result = io.tile([P, N], F32, name="result", bufs=8)
            nc.vector.scalar_tensor_tensor(out=result[:], in0=rows, scalar=factor, in1=acc[:], op0=ALU.mult, op1=ALU.add)
            nc.sync.dma_start(out=out, in_=result[:])

        def next_product(lag=READ_LAG):
            calls[0] += 1
            if issued and calls[0] - issued[0][0] >= lag:
                finish_product()
            if ready and len(issued) < ACC_BANKS:
                issue_product()

        def feature_side(i):
            b, h, j = place(i)
            last = h == H - 1
            slots = slice(j, j + 2)
            if last:
                nc.vector.tensor_reduce(
                    out=n_over_features[:, b, slots], in_=n_over_block[:, b, slots, :], axis=AX.X, op=ALU.add)
            quantize_features(i)
            if last:
                nc.vector.tensor_scalar(
                    out=x_factor[:, b, slots], in0=n_over_features[:, b, slots], scalar1=neg_scale2[:, 0:1],
                    scalar2=None, op0=ALU.mult)
                ready.extend([("out_0", b, j + s, col) for s in range(2) for col in range(0, D, N)])

        def token_side(u):
            b, h = UNITS[u]
            quantize_tokens(u)
            add_token_sums(u)
            if b == B - 1:
                ready.extend([("out_1", h, t, col) for t in range(J) for col in range(0, D, N)])

        with tc.manual_schedule():
            nc.sync.dma_start(out=w_sq_col[:], in_=w_sq.rearrange("(h m t) -> m h t", h=H, t=J))
            nc.sync.dma_start(out=x_sq_raw[:], in_=x_sq.rearrange("b (p j) o -> p b (j o)", j=J))
            nc.sync.dma_start(out=alpha_raw[:], in_=alpha.partition_broadcast(P))
            load_y(0)
            load_y(1)
            load_grad(0)
            load_y(2)
            load_grad(1)
            load_y(3)
            load_grad(2)
            load_grad(3)
            load_weight(0)

            make_identity(nc, ident[:])
            nc.vector.memset(warm[:], 1.0)
            nc.vector.memset(ones[:], 1.0)
            nc.scalar.activation(out=warm[:], in_=warm[:], func=ACT.Exp)
            nc.scalar.activation(out=scale[:], in_=alpha_raw[:], func=ACT.Exp, scale=LOG_BASE)
            nc.scalar.activation(out=warm[:], in_=warm[:], func=ACT.Abs_reciprocal_sqrt)
            nc.vector.tensor_scalar(out=x_sq_eps[:], in0=x_sq_raw[:], scalar1=EPS, scalar2=None, op0=ALU.add)
            spread_w_sq(0)
            make_z(0)
            spread_w_sq(1)
            nc.vector.tensor_scalar(out=scale2[:], in0=scale[:], scalar1=2.0, scalar2=None, op0=ALU.mult)
            nc.vector.tensor_scalar(out=neg_scale2[:], in0=scale[:], scalar1=-2.0, scalar2=None, op0=ALU.mult)
            make_z(1)
            for i in range(2):
                make_q(i)
                square_q(i)
            spread_w_sq(2)
            spread_w_sq(3)

            copied = quantized = 0
            for i in range(STEPS):
                if i + 4 < STEPS:
                    load_y(i + 4)
                    load_grad(i + 4)
                if i < 2 * (H - 1) and i % 2 == 0:
                    load_weight(i // 2 + 1)
                if 0 <= i - 5 < B:
                    load_x(i - 5)
                if i >= STEPS // 2 and i % 2 == 0:
                    load_weight(i // 2 - H)

                if i >= 1:
                    turn(i - 1, 0)
                    turn(i - 1, 1)
                make_r(i)
                if i == 0:
                    make_z(2)
                if i + 2 < STEPS:
                    make_q(i + 2)
                if i >= 2:
                    unit = (i - 2) // 2
                    for t in (2, 3) if i % 2 else (0,):
                        sum_tokens(unit, t)
                if i >= 1:
                    round_dy(i - 1, 0)
                    round_dy(i - 1, 1)
                    turn_back(i - 1)
                if i >= 2 and i % 2 == 0:
                    sum_tokens((i - 2) // 2, 1)
                if i + 2 < STEPS:
                    square_q(i + 2)
                if i + 3 < STEPS:
                    make_z(i + 3)
                make_m(i)
                next_product()
                hold = 0 if i in (WEIGHT_NEEDED, X_NEEDED) else 1
                while quantized < copied - hold:
                    quantize_piece(quantized)
                    quantized += 1
                if i >= 2:
                    feature_side(i - 2)
                if i == STEPS - 1:
                    next_product()
                    feature_side(i - 1)
                next_product()
                if i >= 3 and i % 2 == 1:
                    token_side((i - 3) // 2)
                if i in VECTOR_STEPS:
                    copy_piece(copied, on_vector=True)
                    copied += 1
                make_n(i, 0)
                next_product()
                make_n(i, 1)
                next_product()
                if i >= 2 and i % 2 == 0:
                    gather_slots((i - 2) // 2)
                for k in range(SCALAR_PIECES[i]):
                    copy_piece(copied, on_vector=False)
                    copied += 1
                next_product()

            last = STEPS - 1
            for s in range(2):
                turn(last, s)
            for s in range(2):
                round_dy(last, s)
            for k in range(2):
                next_product(lag=1)
            turn_back(last)
            gather_slots(last // 2)
            for k in range(2):
                next_product(lag=1)
            feature_side(last)
            for k in range(2):
                next_product(lag=1)
            for t in range(J):
                sum_tokens(last // 2, t)
            for k in range(2):
                next_product(lag=1)
            token_side(last // 2)
            while ready or issued:
                next_product(lag=1)
